import numpy as np
import ml_dtypes


def mxq(x, axis, fmt="e4m3"):
    dtype, down = {"e4m3": (ml_dtypes.float8_e4m3fn, 7), "e5m2": (ml_dtypes.float8_e5m2, 14)}[fmt]
    v = np.moveaxis(np.asarray(x, np.float32).astype(ml_dtypes.bfloat16).astype(np.float64), axis, -1)
    blocks = v.reshape(v.shape[:-1] + (-1, 32))
    amax = np.abs(blocks).max(-1, keepdims=True)
    byte = np.maximum(np.where(amax > 0, np.frexp(amax)[1] - 1 + 127, 0) - down, 1)
    scale = np.exp2(byte - 127.0)
    codes = (blocks / scale).astype(np.float32).astype(dtype).astype(np.float64)
    return np.moveaxis((codes * scale).reshape(v.shape), -1, axis)


WIDE = False


def mx_kscale(k):
    if not WIDE:
        return np.ones(k)
    levels = np.array([30, -30])
    if k % 512:
        return np.exp2(np.random.permutation(np.resize(levels, k // 32))).repeat(32)
    a = np.empty((k // 512, 16))
    for p in range(k // 512):
        a[p, :8] = np.random.permutation(np.resize(levels, 8))
        for g in range(8):
            far = levels[np.abs(levels - a[p, g]) >= 10]
            a[p, g + 8] = far[np.random.randint(len(far))]
    return np.exp2(a.ravel()).repeat(32)


BF16 = ml_dtypes.bfloat16


def bf(x):
    return np.asarray(x, np.float32).astype(BF16)


def f64(x):
    return np.asarray(x).astype(np.float64)


B, NH, NW, C, K, P = 2, 8, 8, 512, 1024, 4
T = P * P
HAD = np.array([[1.0, 1.0, 1.0, 1.0],
                [1.0, -1.0, 1.0, -1.0],
                [1.0, 1.0, -1.0, -1.0],
                [1.0, -1.0, -1.0, 1.0]])


def setup_inputs():
    s = mx_kscale(C)
    return {"trans": bf(np.random.standard_normal((T, B, NH, NW, C)) * s),
            "weight": bf(np.random.standard_normal((T, C, K)) * 0.5 * P / np.sqrt(C) / s[:, None]),
            "bias": bf(np.random.standard_normal((1, 1, 1, K)) * 0.2)}


def reference(trans, weight, bias):
    x = f64(trans).reshape(T, B * NH * NW, C)
    y = mxq(x, 2, "e5m2") @ mxq(f64(weight), 1, "e5m2")
    y = y.reshape(P, P, B, NH, NW, K)
    r = np.stack([sum(HAD[p, u] * y[u] for u in range(P)) for p in range(P)])
    z = np.stack([sum(HAD[q, v] * r[:, v] for v in range(P)) for q in range(P)], axis=1) / T
    z = z.transpose(2, 3, 0, 4, 1, 5)
    return z.reshape(B, P * NH, P * NW, K) + f64(bias)

@@ -1,0 +1,362 @@
+from contextlib import ExitStack
+
+import concourse.mybir as mybir
+from concourse.masks import make_identity
+
+F32 = mybir.dt.float32
+BF16 = mybir.dt.bfloat16
+U32 = mybir.dt.uint32
+U8 = mybir.dt.uint8
+MX = mybir.dt.float8_e5m2_x4
+MULT = mybir.AluOpType.mult
+ADD = mybir.AluOpType.add
+SUB = mybir.AluOpType.subtract
+
+P = 128
+COEFFS = 16
+C = 512
+K = 1024
+N = 512
+HALVES = K // N
+STEPS = COEFFS * HALVES
+HAD = ((1, 1, 1, 1), (1, -1, 1, -1), (1, 1, -1, -1), (1, -1, -1, 1))
+FLOPS = 2 * COEFFS * P * C * K
+
+RAW_BUFS = 16
+S_COLS = (256, 256, 320, 320, 320, 320, 320, 320, 320, 320, 320, 320, 320, 320, 320, 320, 416, 416, 416, 416, 448, 448, 448, 448, 448, 448, 448, 448, 448, 448, 448, 448)
+G_COLS = (0,) * 32
+X_AT = (0, 2, 4, 6)
+XQ_AT = (1, 3, 7, 11)
+AHEAD = (1, 1, 1, 1, 1, 1, 2, 2, 2, 2, 3, 4, 5, 5, 6, 6, 6, 5, 4, 4, 3, 3, 2, 2, 2, 2, 2, 2, 2, 1, 1, 0)
+GAP = 1
+CODE_BUFS = 12
+GRP_S_BUFS = 5
+GRP_V_BUFS = 2
+Z_BUFS = 6
+FORM1 = (("v", "v", "v", "v"), ("v", "v", "v", "v"))
+FORM2 = (("pe", "pe", "pe", "pe"), ("pe", "pe", "pe", "pe"))
+RATE = 4
+RATES = {8: 8, 16: 8, 17: 8, 24: 8}
+DEFER_MAX = 2
+PE_LAG = 2
+BIAS_AT = 3
+X_STEPS = (-3, 0, 1, 2)
+FIRST_LOADS = ("x0", 0, 1, "x1", 2, "b", 3, "x2", 4, 5, "x3")
+FINAL_G = 0
+G_WIN = {}
+G_PIECES = 2
+GRP_G_BUFS = 2
+
+
+def tile_iwht3layer_pa_kernel(tc, trans, weight, bias, out):
+    nc = tc.nc
+    x_view = trans.rearrange("t b i j c -> (b i j) t c")
+    w_view = weight.rearrange("t (p r) n -> t p r n", r=4)
+    out_view = out.rearrange("b (i p) (j q) n -> p q (b i) j n", p=4, q=4)
+    bias_row = bias.rearrange("a b c n -> (a b c) n")
+
+    with ExitStack() as ctx:
+        const = ctx.enter_context(tc.tile_pool(name="const", bufs=1))
+        xtmp = ctx.enter_context(tc.tile_pool(name="xtmp", bufs=2))
+        raws = ctx.enter_context(tc.tile_pool(name="raws", bufs=RAW_BUFS))
+        grps_s = ctx.enter_context(tc.tile_pool(name="grps_s", bufs=GRP_S_BUFS))
+        grps_v = ctx.enter_context(tc.tile_pool(name="grps_v", bufs=GRP_V_BUFS))
+        grps_g = ctx.enter_context(tc.tile_pool(name="grps_g", bufs=GRP_G_BUFS))
+        codes = ctx.enter_context(tc.tile_pool(name="codes", bufs=CODE_BUFS))
+        parts = ctx.enter_context(tc.tile_pool(name="parts", bufs=4))
+        wparts = ctx.enter_context(tc.tile_pool(name="wparts", bufs=8))
+        zs = ctx.enter_context(tc.tile_pool(name="zs", bufs=Z_BUFS))
+        psum = ctx.enter_context(tc.psum_pool(name="psum", bufs=1))
+
+        ident = const.tile([P, P], F32, name="ident")
+        ones = const.tile([P, P], BF16, name="ones")
+        bias_pad = const.tile([P, K], BF16, name="bias_pad")
+        bias_sb = const.tile([P, K], F32, name="bias_sb")
+        x_codes = const.tile([P, 4, 1024], U32, name="x_codes", align_bytes=64)
+        x_scales = const.tile([P, 4, 1024], U8, name="x_scales", align_bytes=64)
+
+        def bank(b, shape):
+            return psum.tile(shape, F32, name="bank%d" % b)
+
+        x_raw = {}
+        x_t = {}
+        x_grp = {}
+
+        def load_x(c):
+            x_raw[c] = const.tile([P, 4, C], BF16, name="x_raw%d" % c)
+            nc.sync.dma_start(out=x_raw[c][:], in_=x_view[:, 4 * c : 4 * c + 4, :])
+
+        def transpose_x(c, banks):
+            words = x_raw[c][:].bitcast(F32)
+            x_t[c] = []
+            for pair in range(2):
+                xt = bank(banks[pair], [P, 2, 2, P])
+                x_t[c].append(xt)
+                for tt in range(2):
+                    for u in range(2):
+                        nc.tensor.transpose(xt[:, tt, u, :], words[:, 2 * pair + tt, u : C // 2 : 2], ident[:])
+
+        def copy_x(c):
+            x_grp[c] = const.tile([P, 2, 4, C], BF16, name="x_grp%d" % c, align_bytes=64)
+            for pair in range(2):
+                dst = x_grp[c][:, 0, 2 * pair : 2 * pair + 2, :].bitcast(F32)
+                eng_copy = nc.vector.tensor_copy if (c == 0 and pair == 1) else nc.scalar.copy
+                eng_copy(
+                    out=dst.rearrange("p t (r u) -> p t r u", u=2),
+                    in_=x_t[c][pair][:].rearrange("p t u r -> p t r u"),
+                )
+
+        def negate_x(c):
+            nc.vector.tensor_scalar_mul(
+                out=x_grp[c][:, 1, :, :].rearrange("p t k -> p (t k)"),
+                in0=x_grp[c][:, 0, :, :].rearrange("p t k -> p (t k)"),
+                scalar1=-1.0,
+            )
+
+        def quantize_x(c):
+            nc.vector.quantize_mx(
+                out=x_codes[:, c, :].bitcast(MX),
+                scales=x_scales[:, c, :],
+                in_=x_grp[c][:].rearrange("p s t k -> p (s t k)"),
+            )
+
+        def x_operand(t, sign):
+            lo = (0 if sign > 0 else 512) + (t % 4) * P
+            return x_codes[:, t // 4, lo : lo + P].bitcast(MX), x_scales[:, t // 4, lo : lo + P]
+
+        raw = {}
+        grp = {}
+        w_codes = {}
+        w_scales = {}
+
+        def load_w(s):
+            h, t = divmod(s, COEFFS)
+            raw[s] = raws.tile([P, 4, N], BF16, name="raw")
+            nc.sync.dma_start(out=raw[s][:], in_=w_view[t, :, :, h * N : (h + 1) * N])
+
+        done = set()
+        loaded = [RAW_BUFS]
+
+        def more_loads():
+            while loaded[0] < STEPS and (loaded[0] - RAW_BUFS) in done:
+                load_w(loaded[0])
+                loaded[0] += 1
+
+        def interleave(s):
+            grp[s] = grps_s.tile([P, N, 4], BF16, name="grp", align_bytes=64)
+            a = S_COLS[s]
+            b = N - G_COLS[s]
+            if a > 0:
+                nc.scalar.copy(out=grp[s][:, 0:a, :], in_=raw[s][:, :, 0:a].rearrange("p r n -> p n r"))
+            if b > a:
+                nc.vector.tensor_copy(out=grp[s][:, a:b, :], in_=raw[s][:, :, a:b].rearrange("p r n -> p n r"))
+            if b < N:
+                nc.gpsimd.tensor_scalar(
+                    out=grp[s][:, b:N, :], in0=raw[s][:, :, b:N].rearrange("p r n -> p n r"),
+                    scalar1=1.0, scalar2=0.0, op0=MULT, op1=ADD,
+                )
+            done.add(s)
+            more_loads()
+
+        def pool_piece(s, k):
+            if k == 0:
+                grp[s] = grps_g.tile([P, N, 4], BF16, name="grp_g", align_bytes=64)
+            w = N // G_PIECES
+            cols = slice(k * w, (k + 1) * w)
+            nc.vector.memset(grp[s][:, k * w : k * w + 1, 0:1], 0.0)
+            nc.gpsimd.tensor_scalar(
+                out=grp[s][:, cols, :], in0=raw[s][:, :, cols].rearrange("p r n -> p n r"),
+                scalar1=1.0, scalar2=0.0, op0=MULT, op1=ADD,
+            )
+            if k == G_PIECES - 1:
+                done.add(s)
+                more_loads()
+
+        def quantize_w(s):
+            w_codes[s] = codes.tile([P, N], U32, name="w_codes", align_bytes=64)
+            w_scales[s] = codes.tile([P, N], U8, name="w_scales", align_bytes=64)
+            nc.vector.quantize_mx(
+                out=w_codes[s][:].bitcast(MX),
+                scales=w_scales[s][:],
+                in_=grp[s][:].rearrange("p n r -> p (n r)"),
+            )
+
+        acc = {}
+        base0 = {}
+        s_sum = {}
+        w_sum = {}
+        todo = []
+        waiting = []
+
+        def combine(dst, psum_tile, factor, sb):
+            nc.vector.scalar_tensor_tensor(out=dst, in0=psum_tile[:], scalar=factor, in1=sb, op0=MULT, op1=ADD)
+
+        def store(z, h, q, a, b):
+            p = (0 if a > 0 else 1) + (0 if b > 0 else 2)
+            nc.sync.dma_start(out=out_view[p, q, :, :, h * N : (h + 1) * N], in_=z[:])
+
+        def op_base(h, q, src):
+            base0[q] = parts.tile([P, N], F32, name="base0")
+            combine(base0[q][:], src, 1.0 / 16, bias_sb[:, h * N : (h + 1) * N])
+
+        def op_s(h, q, a, src, from_pe):
+            s_sum[(q, a)] = parts.tile([P, N], F32, name="s_plus" if a > 0 else "s_minus")
+            if from_pe:
+                combine(s_sum[(q, a)][:], src, 1.0 / 16, bias_sb[:, h * N : (h + 1) * N])
+            else:
+                combine(s_sum[(q, a)][:], src, a / 16.0, base0[q][:])
+
+        def op_w(h, q, a, b, src):
+            w_sum[(q, a, b)] = wparts.tile([P, N], F32, name="w_sum")
+            combine(w_sum[(q, a, b)][:], src, b / 16.0, s_sum[(q, a)][:])
+
+        def op_z(h, q, a, b, src, form):
+            z = zs.tile([P, N], F32, name="z")
+            if form == "pe":
+                combine(z[:], src, b / 16.0, s_sum[(q, a)][:])
+            else:
+                combine(z[:], src, a * b / 16.0, w_sum[(q, a, b)][:])
+            store(z, h, q, a, b)
+
+        def op_z_pool(h, q, a, src):
+            t_sb = parts.tile([P, N], F32, name="t_sb")
+            nc.scalar.mul(out=t_sb[:], in_=src[:], mul=1.0 / 16)
+            for b in (1, -1):
+                z = zs.tile([P, N], F32, name="z")
+                nc.gpsimd.tensor_tensor(out=z[:], in0=s_sum[(q, a)][:], in1=t_sb[:], op=ADD if b > 0 else SUB)
+                store(z, h, q, a, b)
+
+        def closed(h, phase, q, j, form, src):
+            b = q + 4 * j
+            a = 1 if j == 0 else -1
+            if phase == 0:
+                if form == "pe":
+                    todo.append((b, lambda: op_s(h, q, a, src, True)))
+                elif j == 0:
+                    todo.append((b, lambda: op_base(h, q, src)))
+                else:
+                    for aa in (1, -1):
+                        todo.append((b, lambda aa=aa: op_s(h, q, aa, src, False)))
+            elif form == "pe":
+                for bb in (1, -1):
+                    todo.append((b, lambda bb=bb: op_z(h, q, a, bb, src, form)))
+            elif j == 0:
+                for aa in (1, -1):
+                    for bb in (1, -1):
+                        todo.append((b, lambda aa=aa, bb=bb: op_w(h, q, aa, bb, src)))
+            else:
+                for aa in (1, -1):
+                    for bb in (1, -1):
+                        todo.append((b, lambda aa=aa, bb=bb: op_z(h, q, aa, bb, src, form)))
+
+        def tile_passes(s):
+            h, t = divmod(s, COEFFS)
+            u, v = divmod(t, 4)
+            phase, uu = divmod(u, 2)
+            res = []
+            for j in range(2):
+                for q in range(4):
+                    form = (FORM1 if phase == 0 else FORM2)[h][q]
+                    if form == "pe":
+                        sign = HAD[q][v] * (-1 if (j == 1 and uu == 1) else 1)
+                        res.append((s, q, j, sign, uu == 0 and v == 0, uu == 1 and v == 3, form))
+                    elif j == uu:
+                        res.append((s, q, j, HAD[q][v], v == 0, v == 3, form))
+            return res
+
+        def emit_pass(item):
+            s, q, j, sign, start, stop, form = item
+            h, t = divmod(s, COEFFS)
+            b = q + 4 * j
+            if start:
+                acc[b] = bank(b, [P, N])
+            lhsT, lhsT_scale = x_operand(t, sign)
+            nc.tensor.matmul_mx(
+                out=acc[b][:], lhsT=lhsT, lhsT_scale=lhsT_scale,
+                rhs=w_codes[s][:].bitcast(MX), rhs_scale=w_scales[s][:],
+                start=start, stop=stop,
+            )
+            if stop:
+                closed(h, t // 8, q, j, form, acc[b])
+
+        freed = {}
+        now = [0]
+
+        def emit_ops(n):
+            for k in range(min(n, len(todo))):
+                b, fn = todo.pop(0)
+                fn()
+                freed[b] = now[0]
+
+        def emit_passes(s):
+            for item in waiting:
+                if item[0] <= s - DEFER_MAX and item[4]:
+                    b = item[1] + 4 * item[2]
+                    idx = [k for k in range(len(todo)) if todo[k][0] == b]
+                    if idx:
+                        emit_ops(idx[-1] + 1)
+            blocked = set()
+            rest = []
+            for item in waiting:
+                b = item[1] + 4 * item[2]
+                if b in blocked or (item[4] and (any(e[0] == b for e in todo) or freed.get(b, -99) + PE_LAG > s)):
+                    blocked.add(b)
+                    rest.append(item)
+                else:
+                    emit_pass(item)
+            waiting.clear()
+            waiting.extend(rest)
+
+        nc.gpsimd.memset(bias_pad[:], 0.0)
+        make_identity(nc, ident[:])
+        nc.gpsimd.memset(ones[:], 1.0)
+        for item in list(FIRST_LOADS) + list(range(6, RAW_BUFS)):
+            if item == "b":
+                nc.sync.dma_start(out=bias_pad[0:1, :], in_=bias_row)
+            elif isinstance(item, str):
+                load_x(int(item[1]))
+            else:
+                load_w(item)
+
+        def bias_to_all():
+            for h in range(HALVES):
+                pb = bank(6 + h, [P, N])
+                nc.tensor.matmul(out=pb[:], lhsT=ones[:], rhs=bias_pad[:, h * N : (h + 1) * N], start=True, stop=True)
+                nc.scalar.copy(out=bias_sb[:, h * N : (h + 1) * N], in_=pb[:])
+
+        made = [0, 0]
+
+        def produce(upto):
+            while made[1] <= min(upto, STEPS - 1):
+                while made[0] <= min(made[1] + GAP, STEPS - 1):
+                    nxt = made[0]
+                    for c in range(4):
+                        if X_AT[c] == nxt:
+                            transpose_x(c, (4, 5) if c % 2 == 0 else (6, 7))
+                            copy_x(c)
+                        if XQ_AT[c] == nxt:
+                            negate_x(c)
+                    interleave(nxt)
+                    for c in range(4):
+                        if XQ_AT[c] == nxt:
+                            quantize_x(c)
+                    if nxt == BIAS_AT:
+                        bias_to_all()
+                    made[0] += 1
+                old = made[1] - CODE_BUFS
+                assert all(item[0] > old for item in waiting), "codes freed too early"
+                quantize_w(made[1])
+                made[1] += 1
+
+        for s in range(STEPS):
+            now[0] = s
+            produce(s + AHEAD[s])
+            emit_ops(RATES.get(s, RATE))
+            waiting.extend(tile_passes(s))
+            emit_passes(s)
+        while todo or waiting:
+            if FINAL_G and not waiting:
+                break
+            emit_ops(len(todo))
+            now[0] += 1
+            emit_passes(STEPS + 99)

@@ -147,9 +147,15 @@ def tile_iwht3layer_pa_kernel(tc, trans, weight, bias, out):
             a = S_COLS[s]
             b = N - G_COLS[s]
             if a > 0:
-                nc.scalar.copy(out=grp[s][:, 0:a, :], in_=raw[s][:, :, 0:a].rearrange("p r n -> p n r"))
+                nc.scalar.copy(
+                    out=grp[s][:, 0:a, :].rearrange("p (c i) r -> p c r i", i=4),
+                    in_=raw[s][:, :, 0:a].rearrange("p r (c i) -> p c r i", i=4),
+                )
             if b > a:
-                nc.vector.tensor_copy(out=grp[s][:, a:b, :], in_=raw[s][:, :, a:b].rearrange("p r n -> p n r"))
+                nc.vector.tensor_copy(
+                    out=grp[s][:, a:b, :].rearrange("p (c i) r -> p c r i", i=4),
+                    in_=raw[s][:, :, a:b].rearrange("p r (c i) -> p c r i", i=4),
+                )
             if b < N:
                 nc.gpsimd.tensor_scalar(
                     out=grp[s][:, b:N, :], in0=raw[s][:, :, b:N].rearrange("p r n -> p n r"),

@@ -23,29 +23,18 @@ HAD = ((1, 1, 1, 1), (1, -1, 1, -1), (1, 1, -1, -1), (1, -1, -1, 1))
 FLOPS = 2 * COEFFS * P * C * K
 
 RAW_BUFS = 16
-S_COLS = (256, 256, 320, 320, 320, 320, 320, 320, 320, 320, 320, 320, 320, 320, 320, 320, 416, 416, 416, 416, 448, 448, 448, 448, 448, 448, 448, 448, 448, 448, 448, 448)
-G_COLS = (0,) * 32
-X_AT = (0, 2, 4, 6)
-XQ_AT = (1, 3, 7, 11)
-AHEAD = (1, 1, 1, 1, 1, 1, 2, 2, 2, 2, 3, 4, 5, 5, 6, 6, 6, 5, 4, 4, 3, 3, 2, 2, 2, 2, 2, 2, 2, 1, 1, 0)
-GAP = 1
-CODE_BUFS = 12
-GRP_S_BUFS = 5
-GRP_V_BUFS = 2
+GRP_BUFS = 5
+CODE_BUFS = 10
 Z_BUFS = 6
+S_COLS = (256, 256, 448, 448, 224, 224, 224, 224, 320, 320, 320, 320, 256, 256, 256, 256, 416, 416, 416, 416, 448, 448, 448, 448, 448, 448, 448, 448, 448, 448, 448, 448)
+G_COLS = (0,) * 32
 FORM1 = (("v", "v", "v", "v"), ("v", "v", "v", "v"))
 FORM2 = (("pe", "pe", "pe", "pe"), ("pe", "pe", "pe", "pe"))
-RATE = 4
-RATES = {8: 8, 16: 8, 17: 8, 24: 8}
-DEFER_MAX = 2
-PE_LAG = 2
-BIAS_AT = 3
-X_STEPS = (-3, 0, 1, 2)
-FIRST_LOADS = ("x0", 0, 1, "x1", 2, "b", 3, "x2", 4, 5, "x3")
-FINAL_G = 0
-G_WIN = {}
-G_PIECES = 2
-GRP_G_BUFS = 2
+LOADS = ("x0", 0, 1, "x1", 2, "b", 3, "x2", 4, 5, "x3")
+X_AT = (0, 1, 2, 3)
+FAST_COPY = 0
+FINAL_POOL = ()
+ORDER = (0, 1, 6, 4, 2, 8, 9, 3, 7, 21, 11, 22, 23, 24, 25, 26, 27, 29, 28, 30, 33, 13, 34, 31, 97, 5, 36, 32, 12, 98, 77, 78, 37, 100, 38, 14, 58, 39, 40, 110, 15, 57, 80, 118, 109, 10, 60, 117, 112, 41, 16, 42, 43, 44, 45, 46, 47, 49, 48, 120, 61, 17, 50, 65, 66, 67, 68, 69, 51, 70, 71, 73, 72, 81, 18, 126, 125, 62, 101, 52, 82, 63, 74, 19, 53, 20, 55, 149, 128, 102, 64, 75, 83, 35, 84, 134, 103, 104, 133, 113, 150, 114, 59, 121, 76, 122, 161, 129, 130, 136, 79, 162, 54, 137, 152, 56, 138, 85, 99, 105, 173, 86, 87, 88, 89, 174, 90, 91, 92, 153, 164, 111, 185, 186, 165, 106, 119, 176, 154, 93, 198, 166, 94, 177, 188, 115, 127, 197, 178, 95, 116, 189, 210, 123, 124, 135, 209, 190, 96, 131, 132, 139, 221, 140, 151, 200, 222, 201, 233, 202, 212, 163, 234, 213, 277, 214, 224, 175, 236, 225, 226, 107, 237, 187, 108, 238, 284, 155, 141, 156, 167, 142, 199, 168, 179, 245, 157, 291, 180, 247, 169, 246, 191, 143, 192, 181, 278, 203, 249, 204, 248, 193, 251, 298, 215, 216, 279, 205, 227, 144, 250, 228, 217, 145, 158, 309, 239, 146, 170, 252, 240, 147, 159, 182, 148, 171, 194, 285, 160, 292, 211, 316, 286, 183, 172, 195, 293, 184, 229, 223, 299, 196, 310, 300, 241, 206, 323, 311, 207, 208, 235, 317, 280, 253, 281, 218, 255, 219, 220, 254, 318, 330, 287, 288, 324, 230, 331, 325, 231, 232, 256, 294, 346, 357, 295, 257, 242, 345, 243, 368, 244, 259, 258, 301, 302, 261, 260, 282, 283, 263, 262, 289, 332, 290, 356, 264, 296, 297, 347, 312, 303, 305, 304, 319, 306, 348, 326, 379, 367, 390, 349, 358, 333, 401, 307, 359, 360, 412, 308, 350, 378, 265, 361, 351, 369, 266, 362, 267, 370, 269, 371, 268, 313, 389, 271, 372, 270, 320, 380, 373, 272, 314, 327, 273, 381, 275, 382, 274, 400, 321, 391, 334, 276, 315, 383, 423, 337, 392, 393, 338, 322, 384, 339, 411, 394, 352, 402, 395, 363, 340, 328, 403, 404, 374, 422, 329, 413, 385, 405, 396, 414, 415, 406, 407, 335, 424, 336, 416, 341, 417, 425, 342, 426, 418, 433, 427, 428, 435, 429, 434, 353, 437, 354, 436, 364, 439, 365, 438, 375, 343, 376, 440, 386, 344, 387, 397, 441, 398, 355, 443, 408, 442, 366, 445, 409, 444, 377, 447, 419, 446, 388, 449, 420, 448, 399, 451, 430, 450, 410, 431, 453, 452, 421, 455, 432, 454, 457, 456, 459, 458, 461, 460, 463, 462, 464)
 
 
 def tile_iwht3layer_pa_kernel(tc, trans, weight, bias, out):
@@ -56,313 +45,215 @@ def tile_iwht3layer_pa_kernel(tc, trans, weight, bias, out):
     bias_row = bias.rearrange("a b c n -> (a b c) n")
 
     with ExitStack() as ctx:
-        const = ctx.enter_context(tc.tile_pool(name="const", bufs=1))
-        xtmp = ctx.enter_context(tc.tile_pool(name="xtmp", bufs=2))
-        raws = ctx.enter_context(tc.tile_pool(name="raws", bufs=RAW_BUFS))
-        grps_s = ctx.enter_context(tc.tile_pool(name="grps_s", bufs=GRP_S_BUFS))
-        grps_v = ctx.enter_context(tc.tile_pool(name="grps_v", bufs=GRP_V_BUFS))
-        grps_g = ctx.enter_context(tc.tile_pool(name="grps_g", bufs=GRP_G_BUFS))
-        codes = ctx.enter_context(tc.tile_pool(name="codes", bufs=CODE_BUFS))
-        parts = ctx.enter_context(tc.tile_pool(name="parts", bufs=4))
-        wparts = ctx.enter_context(tc.tile_pool(name="wparts", bufs=8))
-        zs = ctx.enter_context(tc.tile_pool(name="zs", bufs=Z_BUFS))
+        sbuf = ctx.enter_context(tc.tile_pool(name="sbuf", bufs=1))
         psum = ctx.enter_context(tc.psum_pool(name="psum", bufs=1))
 
-        ident = const.tile([P, P], F32, name="ident")
-        ones = const.tile([P, P], BF16, name="ones")
-        bias_pad = const.tile([P, K], BF16, name="bias_pad")
-        bias_sb = const.tile([P, K], F32, name="bias_sb")
-        x_codes = const.tile([P, 4, 1024], U32, name="x_codes", align_bytes=64)
-        x_scales = const.tile([P, 4, 1024], U8, name="x_scales", align_bytes=64)
+        ident = sbuf.tile([P, P], F32, name="ident")
+        ones = sbuf.tile([P, P], BF16, name="ones")
+        bias_pad = sbuf.tile([P, K], BF16, name="bias_pad")
+        bias_sb = sbuf.tile([P, K], F32, name="bias_sb")
+        x_codes = sbuf.tile([P, 4, 1024], U32, name="x_codes", align_bytes=64)
+        x_scales = sbuf.tile([P, 4, 1024], U8, name="x_scales", align_bytes=64)
+        nc.gpsimd.memset(bias_pad[:], 0.0)
+        make_identity(nc, ident[:])
+        nc.gpsimd.memset(ones[:], 1.0)
+        ctx.enter_context(tc.manual_schedule())
 
-        def bank(b, shape):
-            return psum.tile(shape, F32, name="bank%d" % b)
+        live = {}
+        ops = []
 
-        x_raw = {}
-        x_t = {}
-        x_grp = {}
+        def tile_of(key, pool, shape, dtype, name):
+            if key not in live:
+                live[key] = pool.tile(shape, dtype, name=name, align_bytes=64) if pool is sbuf else pool.tile(shape, dtype, name=name)
+            return live[key]
 
-        def load_x(c):
-            x_raw[c] = const.tile([P, 4, C], BF16, name="x_raw%d" % c)
-            nc.sync.dma_start(out=x_raw[c][:], in_=x_view[:, 4 * c : 4 * c + 4, :])
+        def t_xraw(c):
+            return tile_of(("xraw", c), sbuf, [P, 4, C], BF16, "x_raw%d" % c)
 
-        def transpose_x(c, banks):
-            words = x_raw[c][:].bitcast(F32)
-            x_t[c] = []
+        def t_xgrp(c):
+            return tile_of(("xgrp", c), sbuf, [P, 2, 4, C], BF16, "x_grp%d" % c)
+
+        def t_xt(c, pair):
+            return tile_of(("xt", c, pair), psum, [P, 2, 2, P], F32, "bank%d" % (4 + 2 * (c % 2) + pair))
+
+        def t_raw(s):
+            return tile_of(("raw", s), sbuf, [P, 4, N], BF16, "raw%d" % (s % RAW_BUFS))
+
+        def t_grp(s):
+            return tile_of(("grp", s), sbuf, [P, N, 4], BF16, "grp%d" % (s % GRP_BUFS))
+
+        def t_wc(s):
+            return tile_of(("wc", s), sbuf, [P, N], U32, "w_codes%d" % (s % CODE_BUFS))
+
+        def t_ws(s):
+            return tile_of(("ws", s), sbuf, [P, N], U8, "w_scales%d" % (s % CODE_BUFS))
+
+        def t_acc(h, phase, q, j):
+            return tile_of(("acc", h, phase, q, j), psum, [P, N], F32, "bank%d" % (q + 4 * j))
+
+        def t_part(kind, h, q, a=0, b=0):
+            return tile_of((kind, h, q, a, b), sbuf, [P, N], F32, "%s_%d_%d_%d" % (kind, q, a + 1, b + 1))
+
+        zcount = [0]
+        zslot = {}
+
+        def t_z(h, q, a, b):
+            key = (h, q, a, b)
+            return tile_of(("z",) + key, sbuf, [P, N], F32, "z%d" % zslot[key])
+
+        def op(fn):
+            ops.append(fn)
+
+        def x_chunk(c):
             for pair in range(2):
-                xt = bank(banks[pair], [P, 2, 2, P])
-                x_t[c].append(xt)
                 for tt in range(2):
                     for u in range(2):
-                        nc.tensor.transpose(xt[:, tt, u, :], words[:, 2 * pair + tt, u : C // 2 : 2], ident[:])
-
-        def copy_x(c):
-            x_grp[c] = const.tile([P, 2, 4, C], BF16, name="x_grp%d" % c, align_bytes=64)
+                        op(lambda pair=pair, tt=tt, u=u: nc.tensor.transpose(
+                            t_xt(c, pair)[:, tt, u, :], t_xraw(c)[:].bitcast(F32)[:, 2 * pair + tt, u : C // 2 : 2], ident[:]))
             for pair in range(2):
-                dst = x_grp[c][:, 0, 2 * pair : 2 * pair + 2, :].bitcast(F32)
                 eng_copy = nc.vector.tensor_copy if (c == 0 and pair == 1) else nc.scalar.copy
-                eng_copy(
-                    out=dst.rearrange("p t (r u) -> p t r u", u=2),
-                    in_=x_t[c][pair][:].rearrange("p t u r -> p t r u"),
-                )
-
-        def negate_x(c):
-            nc.vector.tensor_scalar_mul(
-                out=x_grp[c][:, 1, :, :].rearrange("p t k -> p (t k)"),
-                in0=x_grp[c][:, 0, :, :].rearrange("p t k -> p (t k)"),
-                scalar1=-1.0,
-            )
-
-        def quantize_x(c):
-            nc.vector.quantize_mx(
-                out=x_codes[:, c, :].bitcast(MX),
-                scales=x_scales[:, c, :],
-                in_=x_grp[c][:].rearrange("p s t k -> p (s t k)"),
-            )
+                op(lambda pair=pair, eng_copy=eng_copy: eng_copy(
+                    out=t_xgrp(c)[:, 0, 2 * pair : 2 * pair + 2, :].bitcast(F32).rearrange("p t (r u) -> p t r u", u=2),
+                    in_=t_xt(c, pair)[:].rearrange("p t u r -> p t r u")))
+            op(lambda: nc.vector.tensor_scalar_mul(
+                out=t_xgrp(c)[:, 1, :, :].rearrange("p t k -> p (t k)"),
+                in0=t_xgrp(c)[:, 0, :, :].rearrange("p t k -> p (t k)"), scalar1=-1.0))
+            op(lambda: nc.vector.quantize_mx(
+                out=x_codes[:, c, :].bitcast(MX), scales=x_scales[:, c, :],
+                in_=t_xgrp(c)[:].rearrange("p s t k -> p (s t k)")))
 
         def x_operand(t, sign):
             lo = (0 if sign > 0 else 512) + (t % 4) * P
             return x_codes[:, t // 4, lo : lo + P].bitcast(MX), x_scales[:, t // 4, lo : lo + P]
 
-        raw = {}
-        grp = {}
-        w_codes = {}
-        w_scales = {}
+        def bias_to_all():
+            for h in range(HALVES):
+                key = ("pb", h)
+                op(lambda h=h, key=key: nc.tensor.matmul(
+                    out=tile_of(key, psum, [P, N], F32, "bank%d" % (6 + h))[:], lhsT=ones[:],
+                    rhs=bias_pad[:, h * N : (h + 1) * N], start=True, stop=True))
+                op(lambda h=h, key=key: nc.scalar.copy(out=bias_sb[:, h * N : (h + 1) * N], in_=live[key][:]))
 
         def load_w(s):
             h, t = divmod(s, COEFFS)
-            raw[s] = raws.tile([P, 4, N], BF16, name="raw")
-            nc.sync.dma_start(out=raw[s][:], in_=w_view[t, :, :, h * N : (h + 1) * N])
+            op(lambda: nc.sync.dma_start(out=t_raw(s)[:], in_=w_view[t, :, :, h * N : (h + 1) * N]))
 
-        done = set()
-        loaded = [RAW_BUFS]
+        def views(s, lo, hi):
+            if FAST_COPY:
+                return (t_grp(s)[:, lo:hi, :].rearrange("p (c i) r -> p c r i", i=4),
+                        t_raw(s)[:, :, lo:hi].rearrange("p r (c i) -> p c r i", i=4))
+            return t_grp(s)[:, lo:hi, :], t_raw(s)[:, :, lo:hi].rearrange("p r n -> p n r")
 
-        def more_loads():
-            while loaded[0] < STEPS and (loaded[0] - RAW_BUFS) in done:
-                load_w(loaded[0])
-                loaded[0] += 1
+        def s_part(s, lo, hi):
+            dst, src = views(s, lo, hi)
+            nc.scalar.copy(out=dst, in_=src)
 
-        def interleave(s):
-            grp[s] = grps_s.tile([P, N, 4], BF16, name="grp", align_bytes=64)
+        def v_part(s, lo, hi):
+            dst, src = views(s, lo, hi)
+            nc.vector.tensor_copy(out=dst, in_=src)
+
+        def g_part(s, lo, hi):
+            nc.gpsimd.tensor_scalar(out=t_grp(s)[:, lo:hi, :], in0=t_raw(s)[:, :, lo:hi].rearrange("p r n -> p n r"),
+                                    scalar1=1.0, scalar2=0.0, op0=MULT, op1=ADD)
+
+        def produce(s):
             a = S_COLS[s]
             b = N - G_COLS[s]
             if a > 0:
-                nc.scalar.copy(
-                    out=grp[s][:, 0:a, :].rearrange("p (c i) r -> p c r i", i=4),
-                    in_=raw[s][:, :, 0:a].rearrange("p r (c i) -> p c r i", i=4),
-                )
+                op(lambda: s_part(s, 0, a))
             if b > a:
-                nc.vector.tensor_copy(
-                    out=grp[s][:, a:b, :].rearrange("p (c i) r -> p c r i", i=4),
-                    in_=raw[s][:, :, a:b].rearrange("p r (c i) -> p c r i", i=4),
-                )
+                op(lambda: v_part(s, a, b))
             if b < N:
-                nc.gpsimd.tensor_scalar(
-                    out=grp[s][:, b:N, :], in0=raw[s][:, :, b:N].rearrange("p r n -> p n r"),
-                    scalar1=1.0, scalar2=0.0, op0=MULT, op1=ADD,
-                )
-            done.add(s)
-            more_loads()
+                op(lambda: g_part(s, b, N))
+            if s + RAW_BUFS < STEPS:
+                load_w(s + RAW_BUFS)
+            op(lambda: nc.vector.quantize_mx(out=t_wc(s)[:].bitcast(MX), scales=t_ws(s)[:],
+                                             in_=t_grp(s)[:].rearrange("p n r -> p (n r)")))
 
-        def pool_piece(s, k):
-            if k == 0:
-                grp[s] = grps_g.tile([P, N, 4], BF16, name="grp_g", align_bytes=64)
-            w = N // G_PIECES
-            cols = slice(k * w, (k + 1) * w)
-            nc.vector.memset(grp[s][:, k * w : k * w + 1, 0:1], 0.0)
-            nc.gpsimd.tensor_scalar(
-                out=grp[s][:, cols, :], in0=raw[s][:, :, cols].rearrange("p r n -> p n r"),
-                scalar1=1.0, scalar2=0.0, op0=MULT, op1=ADD,
-            )
-            if k == G_PIECES - 1:
-                done.add(s)
-                more_loads()
+        def combine(dst, src, factor, sb):
+            nc.vector.scalar_tensor_tensor(out=dst[:], in0=src[:], scalar=factor, in1=sb, op0=MULT, op1=ADD)
 
-        def quantize_w(s):
-            w_codes[s] = codes.tile([P, N], U32, name="w_codes", align_bytes=64)
-            w_scales[s] = codes.tile([P, N], U8, name="w_scales", align_bytes=64)
-            nc.vector.quantize_mx(
-                out=w_codes[s][:].bitcast(MX),
-                scales=w_scales[s][:],
-                in_=grp[s][:].rearrange("p n r -> p (n r)"),
-            )
-
-        acc = {}
-        base0 = {}
-        s_sum = {}
-        w_sum = {}
-        todo = []
-        waiting = []
-
-        def combine(dst, psum_tile, factor, sb):
-            nc.vector.scalar_tensor_tensor(out=dst, in0=psum_tile[:], scalar=factor, in1=sb, op0=MULT, op1=ADD)
-
-        def store(z, h, q, a, b):
+        def store(h, q, a, b):
+            zslot[(h, q, a, b)] = zcount[0] % Z_BUFS
+            zcount[0] += 1
             p = (0 if a > 0 else 1) + (0 if b > 0 else 2)
-            nc.sync.dma_start(out=out_view[p, q, :, :, h * N : (h + 1) * N], in_=z[:])
+            op(lambda: nc.sync.dma_start(out=out_view[p, q, :, :, h * N : (h + 1) * N], in_=t_z(h, q, a, b)[:]))
 
-        def op_base(h, q, src):
-            base0[q] = parts.tile([P, N], F32, name="base0")
-            combine(base0[q][:], src, 1.0 / 16, bias_sb[:, h * N : (h + 1) * N])
-
-        def op_s(h, q, a, src, from_pe):
-            s_sum[(q, a)] = parts.tile([P, N], F32, name="s_plus" if a > 0 else "s_minus")
-            if from_pe:
-                combine(s_sum[(q, a)][:], src, 1.0 / 16, bias_sb[:, h * N : (h + 1) * N])
-            else:
-                combine(s_sum[(q, a)][:], src, a / 16.0, base0[q][:])
-
-        def op_w(h, q, a, b, src):
-            w_sum[(q, a, b)] = wparts.tile([P, N], F32, name="w_sum")
-            combine(w_sum[(q, a, b)][:], src, b / 16.0, s_sum[(q, a)][:])
-
-        def op_z(h, q, a, b, src, form):
-            z = zs.tile([P, N], F32, name="z")
-            if form == "pe":
-                combine(z[:], src, b / 16.0, s_sum[(q, a)][:])
-            else:
-                combine(z[:], src, a * b / 16.0, w_sum[(q, a, b)][:])
-            store(z, h, q, a, b)
-
-        def op_z_pool(h, q, a, src):
-            t_sb = parts.tile([P, N], F32, name="t_sb")
-            nc.scalar.mul(out=t_sb[:], in_=src[:], mul=1.0 / 16)
-            for b in (1, -1):
-                z = zs.tile([P, N], F32, name="z")
-                nc.gpsimd.tensor_tensor(out=z[:], in0=s_sum[(q, a)][:], in1=t_sb[:], op=ADD if b > 0 else SUB)
-                store(z, h, q, a, b)
-
-        def closed(h, phase, q, j, form, src):
-            b = q + 4 * j
+        def closed(h, phase, q, j, form):
             a = 1 if j == 0 else -1
+            cols = slice(h * N, (h + 1) * N)
+            src = lambda: t_acc(h, phase, q, j)
             if phase == 0:
                 if form == "pe":
-                    todo.append((b, lambda: op_s(h, q, a, src, True)))
+                    op(lambda: combine(t_part("s", h, q, a), src(), 1.0 / 16, bias_sb[:, cols]))
                 elif j == 0:
-                    todo.append((b, lambda: op_base(h, q, src)))
+                    op(lambda: combine(t_part("base", h, q), src(), 1.0 / 16, bias_sb[:, cols]))
                 else:
                     for aa in (1, -1):
-                        todo.append((b, lambda aa=aa: op_s(h, q, aa, src, False)))
+                        op(lambda aa=aa: combine(t_part("s", h, q, aa), src(), aa / 16.0, t_part("base", h, q)[:]))
             elif form == "pe":
-                for bb in (1, -1):
-                    todo.append((b, lambda bb=bb: op_z(h, q, a, bb, src, form)))
+                if h == HALVES - 1 and (q + 4 * j) in FINAL_POOL:
+                    op(lambda: nc.scalar.mul(out=t_part("t", h, q, a)[:], in_=src()[:], mul=1.0 / 16))
+                    for bb in (1, -1):
+                        op(lambda bb=bb: nc.gpsimd.tensor_tensor(out=t_z(h, q, a, bb)[:], in0=t_part("s", h, q, a)[:],
+                                                                 in1=t_part("t", h, q, a)[:], op=ADD if bb > 0 else SUB))
+                        store(h, q, a, bb)
+                else:
+                    for bb in (1, -1):
+                        op(lambda bb=bb: combine(t_z(h, q, a, bb), src(), bb / 16.0, t_part("s", h, q, a)[:]))
+                        store(h, q, a, bb)
             elif j == 0:
                 for aa in (1, -1):
                     for bb in (1, -1):
-                        todo.append((b, lambda aa=aa, bb=bb: op_w(h, q, aa, bb, src)))
+                        op(lambda aa=aa, bb=bb: combine(t_part("w", h, q, aa, bb), src(), bb / 16.0, t_part("s", h, q, aa)[:]))
             else:
                 for aa in (1, -1):
                     for bb in (1, -1):
-                        todo.append((b, lambda aa=aa, bb=bb: op_z(h, q, aa, bb, src, form)))
+                        op(lambda aa=aa, bb=bb: combine(t_z(h, q, aa, bb), src(), aa * bb / 16.0, t_part("w", h, q, aa, bb)[:]))
+                        store(h, q, aa, bb)
 
-        def tile_passes(s):
+        def one_pass(s, q, j, sign, start, stop):
+            h, t = divmod(s, COEFFS)
+            lhsT, lhsT_scale = x_operand(t, sign)
+            nc.tensor.matmul_mx(out=t_acc(h, t // 8, q, j)[:], lhsT=lhsT, lhsT_scale=lhsT_scale,
+                                rhs=t_wc(s)[:].bitcast(MX), rhs_scale=t_ws(s)[:], start=start, stop=stop)
+
+        def passes(s):
             h, t = divmod(s, COEFFS)
             u, v = divmod(t, 4)
             phase, uu = divmod(u, 2)
-            res = []
+            ends = []
             for j in range(2):
                 for q in range(4):
                     form = (FORM1 if phase == 0 else FORM2)[h][q]
                     if form == "pe":
                         sign = HAD[q][v] * (-1 if (j == 1 and uu == 1) else 1)
-                        res.append((s, q, j, sign, uu == 0 and v == 0, uu == 1 and v == 3, form))
+                        start, stop = uu == 0 and v == 0, uu == 1 and v == 3
                     elif j == uu:
-                        res.append((s, q, j, HAD[q][v], v == 0, v == 3, form))
-            return res
+                        sign, start, stop = HAD[q][v], v == 0, v == 3
+                    else:
+                        continue
+                    op(lambda q=q, j=j, sign=sign, start=start, stop=stop: one_pass(s, q, j, sign, start, stop))
+                    if stop:
+                        ends.append((h, phase, q, j, form))
+            for e in ends:
+                closed(e[0], e[1], e[2], e[3], e[4])
 
-        def emit_pass(item):
-            s, q, j, sign, start, stop, form = item
-            h, t = divmod(s, COEFFS)
-            b = q + 4 * j
-            if start:
-                acc[b] = bank(b, [P, N])
-            lhsT, lhsT_scale = x_operand(t, sign)
-            nc.tensor.matmul_mx(
-                out=acc[b][:], lhsT=lhsT, lhsT_scale=lhsT_scale,
-                rhs=w_codes[s][:].bitcast(MX), rhs_scale=w_scales[s][:],
-                start=start, stop=stop,
-            )
-            if stop:
-                closed(h, t // 8, q, j, form, acc[b])
-
-        freed = {}
-        now = [0]
-
-        def emit_ops(n):
-            for k in range(min(n, len(todo))):
-                b, fn = todo.pop(0)
-                fn()
-                freed[b] = now[0]
-
-        def emit_passes(s):
-            for item in waiting:
-                if item[0] <= s - DEFER_MAX and item[4]:
-                    b = item[1] + 4 * item[2]
-                    idx = [k for k in range(len(todo)) if todo[k][0] == b]
-                    if idx:
-                        emit_ops(idx[-1] + 1)
-            blocked = set()
-            rest = []
-            for item in waiting:
-                b = item[1] + 4 * item[2]
-                if b in blocked or (item[4] and (any(e[0] == b for e in todo) or freed.get(b, -99) + PE_LAG > s)):
-                    blocked.add(b)
-                    rest.append(item)
-                else:
-                    emit_pass(item)
-            waiting.clear()
-            waiting.extend(rest)
-
-        nc.gpsimd.memset(bias_pad[:], 0.0)
-        make_identity(nc, ident[:])
-        nc.gpsimd.memset(ones[:], 1.0)
-        for item in list(FIRST_LOADS) + list(range(6, RAW_BUFS)):
+        for item in list(LOADS) + list(range(6, RAW_BUFS)):
             if item == "b":
-                nc.sync.dma_start(out=bias_pad[0:1, :], in_=bias_row)
+                op(lambda: nc.sync.dma_start(out=bias_pad[0:1, :], in_=bias_row))
             elif isinstance(item, str):
-                load_x(int(item[1]))
+                op(lambda c=int(item[1]): nc.sync.dma_start(out=t_xraw(c)[:], in_=x_view[:, 4 * c : 4 * c + 4, :]))
             else:
                 load_w(item)
-
-        def bias_to_all():
-            for h in range(HALVES):
-                pb = bank(6 + h, [P, N])
-                nc.tensor.matmul(out=pb[:], lhsT=ones[:], rhs=bias_pad[:, h * N : (h + 1) * N], start=True, stop=True)
-                nc.scalar.copy(out=bias_sb[:, h * N : (h + 1) * N], in_=pb[:])
-
-        made = [0, 0]
-
-        def produce(upto):
-            while made[1] <= min(upto, STEPS - 1):
-                while made[0] <= min(made[1] + GAP, STEPS - 1):
-                    nxt = made[0]
-                    for c in range(4):
-                        if X_AT[c] == nxt:
-                            transpose_x(c, (4, 5) if c % 2 == 0 else (6, 7))
-                            copy_x(c)
-                        if XQ_AT[c] == nxt:
-                            negate_x(c)
-                    interleave(nxt)
-                    for c in range(4):
-                        if XQ_AT[c] == nxt:
-                            quantize_x(c)
-                    if nxt == BIAS_AT:
-                        bias_to_all()
-                    made[0] += 1
-                old = made[1] - CODE_BUFS
-                assert all(item[0] > old for item in waiting), "codes freed too early"
-                quantize_w(made[1])
-                made[1] += 1
-
         for s in range(STEPS):
-            now[0] = s
-            produce(s + AHEAD[s])
-            emit_ops(RATES.get(s, RATE))
-            waiting.extend(tile_passes(s))
-            emit_passes(s)
-        while todo or waiting:
-            if FINAL_G and not waiting:
-                break
-            emit_ops(len(todo))
-            now[0] += 1
-            emit_passes(STEPS + 99)
+            for c in range(4):
+                if X_AT[c] == s:
+                    x_chunk(c)
+                    if c == 1:
+                        bias_to_all()
+            produce(s)
+            passes(s)
+
+        for k in (ORDER if ORDER else range(len(ops))):
+            ops[k]()

@@ -32,9 +32,10 @@ FORM1 = (("v", "v", "v", "v"), ("v", "v", "v", "v"))
 FORM2 = (("pe", "pe", "pe", "pe"), ("pe", "pe", "pe", "pe"))
 LOADS = ("x0", 0, 1, "x1", 2, "b", 3, "x2", 4, 5, "x3")
 X_AT = (0, 1, 2, 3)
+X_BANKS = ((4, 5), (6, 7), (4, 5), (6, 7))
 FAST_COPY = 0
 FINAL_POOL = ()
-ORDER = (0, 1, 6, 4, 2, 8, 9, 3, 7, 21, 11, 22, 23, 24, 25, 26, 27, 29, 28, 30, 33, 13, 34, 31, 97, 5, 36, 32, 12, 98, 77, 78, 37, 100, 38, 14, 58, 39, 40, 110, 15, 57, 80, 118, 109, 10, 60, 117, 112, 41, 16, 42, 43, 44, 45, 46, 47, 49, 48, 120, 61, 17, 50, 65, 66, 67, 68, 69, 51, 70, 71, 73, 72, 81, 18, 126, 125, 62, 101, 52, 82, 63, 74, 19, 53, 20, 55, 149, 128, 102, 64, 75, 83, 35, 84, 134, 103, 104, 133, 113, 150, 114, 59, 121, 76, 122, 161, 129, 130, 136, 79, 162, 54, 137, 152, 56, 138, 85, 99, 105, 173, 86, 87, 88, 89, 174, 90, 91, 92, 153, 164, 111, 185, 186, 165, 106, 119, 176, 154, 93, 198, 166, 94, 177, 188, 115, 127, 197, 178, 95, 116, 189, 210, 123, 124, 135, 209, 190, 96, 131, 132, 139, 221, 140, 151, 200, 222, 201, 233, 202, 212, 163, 234, 213, 277, 214, 224, 175, 236, 225, 226, 107, 237, 187, 108, 238, 284, 155, 141, 156, 167, 142, 199, 168, 179, 245, 157, 291, 180, 247, 169, 246, 191, 143, 192, 181, 278, 203, 249, 204, 248, 193, 251, 298, 215, 216, 279, 205, 227, 144, 250, 228, 217, 145, 158, 309, 239, 146, 170, 252, 240, 147, 159, 182, 148, 171, 194, 285, 160, 292, 211, 316, 286, 183, 172, 195, 293, 184, 229, 223, 299, 196, 310, 300, 241, 206, 323, 311, 207, 208, 235, 317, 280, 253, 281, 218, 255, 219, 220, 254, 318, 330, 287, 288, 324, 230, 331, 325, 231, 232, 256, 294, 346, 357, 295, 257, 242, 345, 243, 368, 244, 259, 258, 301, 302, 261, 260, 282, 283, 263, 262, 289, 332, 290, 356, 264, 296, 297, 347, 312, 303, 305, 304, 319, 306, 348, 326, 379, 367, 390, 349, 358, 333, 401, 307, 359, 360, 412, 308, 350, 378, 265, 361, 351, 369, 266, 362, 267, 370, 269, 371, 268, 313, 389, 271, 372, 270, 320, 380, 373, 272, 314, 327, 273, 381, 275, 382, 274, 400, 321, 391, 334, 276, 315, 383, 423, 337, 392, 393, 338, 322, 384, 339, 411, 394, 352, 402, 395, 363, 340, 328, 403, 404, 374, 422, 329, 413, 385, 405, 396, 414, 415, 406, 407, 335, 424, 336, 416, 341, 417, 425, 342, 426, 418, 433, 427, 428, 435, 429, 434, 353, 437, 354, 436, 364, 439, 365, 438, 375, 343, 376, 440, 386, 344, 387, 397, 441, 398, 355, 443, 408, 442, 366, 445, 409, 444, 377, 447, 419, 446, 388, 449, 420, 448, 399, 451, 430, 450, 410, 431, 453, 452, 421, 455, 432, 454, 457, 456, 459, 458, 461, 460, 463, 462, 464)
+ORDER = (0, 1, 6, 4, 2, 8, 9, 3, 7, 22, 21, 23, 24, 27, 28, 25, 29, 26, 11, 33, 34, 30, 5, 97, 13, 78, 31, 77, 98, 32, 14, 36, 58, 57, 10, 38, 100, 37, 40, 80, 39, 109, 12, 110, 117, 60, 118, 15, 44, 43, 41, 112, 42, 48, 45, 46, 49, 47, 120, 16, 50, 66, 68, 65, 67, 70, 69, 72, 51, 73, 71, 74, 17, 126, 53, 18, 61, 125, 64, 52, 55, 19, 56, 150, 54, 113, 75, 62, 149, 81, 20, 128, 114, 82, 76, 102, 161, 35, 90, 162, 63, 106, 101, 86, 121, 152, 79, 133, 87, 105, 84, 91, 134, 88, 122, 111, 173, 154, 164, 104, 153, 174, 92, 165, 136, 59, 83, 185, 186, 89, 85, 103, 176, 166, 99, 198, 94, 177, 130, 93, 188, 197, 127, 95, 115, 129, 178, 210, 116, 209, 137, 200, 138, 119, 190, 96, 124, 221, 189, 132, 123, 212, 131, 233, 222, 202, 201, 234, 213, 277, 214, 224, 140, 139, 236, 225, 107, 226, 237, 108, 238, 291, 155, 141, 156, 167, 142, 168, 179, 146, 157, 309, 144, 191, 180, 143, 169, 192, 145, 181, 158, 148, 193, 170, 284, 249, 203, 159, 299, 204, 147, 182, 215, 251, 171, 160, 298, 292, 183, 252, 285, 175, 194, 135, 151, 278, 205, 286, 172, 227, 279, 217, 239, 323, 245, 206, 216, 310, 184, 255, 246, 163, 195, 223, 196, 253, 229, 281, 247, 316, 228, 241, 311, 248, 280, 187, 256, 240, 293, 282, 287, 324, 259, 218, 199, 289, 330, 257, 294, 208, 300, 207, 230, 211, 331, 220, 263, 219, 254, 242, 346, 301, 261, 345, 296, 231, 317, 332, 283, 260, 288, 318, 243, 312, 325, 295, 356, 232, 368, 319, 235, 357, 302, 305, 290, 258, 326, 347, 244, 297, 306, 303, 367, 348, 358, 304, 349, 307, 359, 308, 350, 333, 265, 378, 360, 351, 369, 361, 362, 267, 371, 271, 370, 268, 372, 264, 379, 313, 389, 269, 373, 320, 390, 380, 270, 314, 272, 266, 327, 275, 321, 384, 273, 334, 400, 382, 391, 383, 274, 276, 315, 401, 381, 250, 338, 328, 394, 337, 262, 322, 393, 411, 412, 392, 339, 352, 402, 329, 335, 340, 363, 395, 342, 403, 422, 374, 341, 406, 385, 413, 336, 404, 423, 396, 343, 353, 415, 414, 424, 407, 405, 344, 417, 425, 416, 426, 435, 354, 364, 433, 436, 428, 365, 437, 434, 427, 439, 375, 438, 418, 441, 376, 440, 386, 443, 355, 442, 387, 445, 397, 444, 366, 447, 398, 446, 408, 429, 448, 377, 419, 449, 388, 430, 451, 450, 409, 399, 453, 452, 420, 410, 455, 454, 431, 421, 456, 457, 432, 459, 458, 461, 460, 463, 462, 464)
 
 
 def tile_iwht3layer_pa_kernel(tc, trans, weight, bias, out):
@@ -74,7 +75,7 @@ def tile_iwht3layer_pa_kernel(tc, trans, weight, bias, out):
             return tile_of(("xgrp", c), sbuf, [P, 2, 4, C], BF16, "x_grp%d" % c)
 
         def t_xt(c, pair):
-            return tile_of(("xt", c, pair), psum, [P, 2, 2, P], F32, "bank%d" % (4 + 2 * (c % 2) + pair))
+            return tile_of(("xt", c, pair), psum, [P, 2, 2, P], F32, "bank%d" % X_BANKS[c][pair])
 
         def t_raw(s):
             return tile_of(("raw", s), sbuf, [P, 4, N], BF16, "raw%d" % (s % RAW_BUFS))
@@ -98,8 +99,8 @@ def tile_iwht3layer_pa_kernel(tc, trans, weight, bias, out):
         zslot = {}
 
         def t_z(h, q, a, b):
-            key = (h, q, a, b)
-            return tile_of(("z",) + key, sbuf, [P, N], F32, "z%d" % zslot[key])
+            k = zslot[(h, q, a, b)]
+            return tile_of(("z", h, k // 4), sbuf, [P, 4, N], F32, "x_grp%d" % (k // 4))[:, k % 4, :]
 
         def op(fn):
             ops.append(fn)
@@ -171,13 +172,13 @@ def tile_iwht3layer_pa_kernel(tc, trans, weight, bias, out):
                                              in_=t_grp(s)[:].rearrange("p n r -> p (n r)")))
 
         def combine(dst, src, factor, sb):
-            nc.vector.scalar_tensor_tensor(out=dst[:], in0=src[:], scalar=factor, in1=sb, op0=MULT, op1=ADD)
+            nc.vector.scalar_tensor_tensor(out=dst, in0=src[:], scalar=factor, in1=sb, op0=MULT, op1=ADD)
 
         def store(h, q, a, b):
-            zslot[(h, q, a, b)] = zcount[0] % Z_BUFS
+            zslot[(h, q, a, b)] = zcount[0] % 16
             zcount[0] += 1
             p = (0 if a > 0 else 1) + (0 if b > 0 else 2)
-            op(lambda: nc.sync.dma_start(out=out_view[p, q, :, :, h * N : (h + 1) * N], in_=t_z(h, q, a, b)[:]))
+            op(lambda: nc.sync.dma_start(out=out_view[p, q, :, :, h * N : (h + 1) * N], in_=t_z(h, q, a, b)))
 
         def closed(h, phase, q, j, form):
             a = 1 if j == 0 else -1
@@ -185,17 +186,17 @@ def tile_iwht3layer_pa_kernel(tc, trans, weight, bias, out):
             src = lambda: t_acc(h, phase, q, j)
             if phase == 0:
                 if form == "pe":
-                    op(lambda: combine(t_part("s", h, q, a), src(), 1.0 / 16, bias_sb[:, cols]))
+                    op(lambda: combine(t_part("s", h, q, a)[:], src(), 1.0 / 16, bias_sb[:, cols]))
                 elif j == 0:
-                    op(lambda: combine(t_part("base", h, q), src(), 1.0 / 16, bias_sb[:, cols]))
+                    op(lambda: combine(t_part("base", h, q)[:], src(), 1.0 / 16, bias_sb[:, cols]))
                 else:
                     for aa in (1, -1):
-                        op(lambda aa=aa: combine(t_part("s", h, q, aa), src(), aa / 16.0, t_part("base", h, q)[:]))
+                        op(lambda aa=aa: combine(t_part("s", h, q, aa)[:], src(), aa / 16.0, t_part("base", h, q)[:]))
             elif form == "pe":
                 if h == HALVES - 1 and (q + 4 * j) in FINAL_POOL:
                     op(lambda: nc.scalar.mul(out=t_part("t", h, q, a)[:], in_=src()[:], mul=1.0 / 16))
                     for bb in (1, -1):
-                        op(lambda bb=bb: nc.gpsimd.tensor_tensor(out=t_z(h, q, a, bb)[:], in0=t_part("s", h, q, a)[:],
+                        op(lambda bb=bb: nc.gpsimd.tensor_tensor(out=t_z(h, q, a, bb), in0=t_part("s", h, q, a)[:],
                                                                  in1=t_part("t", h, q, a)[:], op=ADD if bb > 0 else SUB))
                         store(h, q, a, bb)
                 else:
@@ -205,7 +206,7 @@ def tile_iwht3layer_pa_kernel(tc, trans, weight, bias, out):
             elif j == 0:
                 for aa in (1, -1):
                     for bb in (1, -1):
-                        op(lambda aa=aa, bb=bb: combine(t_part("w", h, q, aa, bb), src(), bb / 16.0, t_part("s", h, q, aa)[:]))
+                        op(lambda aa=aa, bb=bb: combine(t_part("w", h, q, aa, bb)[:], src(), bb / 16.0, t_part("s", h, q, aa)[:]))
             else:
                 for aa in (1, -1):
                     for bb in (1, -1):

@@ -7,35 +7,45 @@ F32 = mybir.dt.float32
 BF16 = mybir.dt.bfloat16
 U32 = mybir.dt.uint32
 U8 = mybir.dt.uint8
-MX = mybir.dt.float8_e5m2_x4
+E5M2_X4 = mybir.dt.float8_e5m2_x4
 MULT = mybir.AluOpType.mult
 ADD = mybir.AluOpType.add
-SUB = mybir.AluOpType.subtract
 
 P = 128
 COEFFS = 16
-C = 512
-K = 1024
+C_IN = 512
+C_OUT = 1024
 N = 512
-HALVES = K // N
-STEPS = COEFFS * HALVES
+HALVES = C_OUT // N
+TILES = COEFFS * HALVES
 HAD = ((1, 1, 1, 1), (1, -1, 1, -1), (1, 1, -1, -1), (1, -1, -1, 1))
-FLOPS = 2 * COEFFS * P * C * K
+FLOPS = 2 * COEFFS * P * C_IN * C_OUT
 
-RAW_BUFS = 16
-GRP_BUFS = 5
-CODE_BUFS = 10
-Z_BUFS = 6
-S_COLS = (256, 256, 448, 448, 224, 224, 224, 224, 320, 320, 320, 320, 256, 256, 256, 256, 416, 416, 416, 416, 448, 448, 448, 448, 448, 448, 448, 448, 448, 448, 448, 448)
-G_COLS = (0,) * 32
-FORM1 = (("v", "v", "v", "v"), ("v", "v", "v", "v"))
-FORM2 = (("pe", "pe", "pe", "pe"), ("pe", "pe", "pe", "pe"))
-LOADS = ("x0", 0, 1, "x1", 2, "b", 3, "x2", 4, 5, "x3")
-X_AT = (0, 1, 2, 3)
+RAW_SLOTS = 16
+GROUPED_SLOTS = 5
+CODE_SLOTS = 10
+
+VECTOR_TILES = (1, 4, 6, 9, 12, 16, 17, 25, 28)
+
+LAG = (
+    (((-2.0, 0.75, 0.5, 0.0), (-1.5, -0.75, 2.0, 1.5)), ((-1.75, -1.5, -1.5, -2.0), (0.25, 1.0, 3.75, 3.25))),
+    (((1.0, 2.5, 2.5, 2.25), (1.0, -0.5, 4.0, 2.0)), ((1.25, 1.5, 1.5, 1.25), (7.0, 5.25, 11.25, 13.75))),
+)
+AHEAD = (2.5, 2.75, 1.25, 1.75, 2.0, 2.25, 2.75, 3.25)
+COPY_BEFORE = 1.5
+SUM_AFTER = (0.75, 2.25, 2.25)
+X_LOAD_AT = (-5.5, 2.75, 6.0, 10.0)
+X_TURN_AT = (-11.75, -6.5, 1.75, 4.25)
+X_COPY_AT = (-5.0, 2.5, 6.0, 8.25)
+X_COPY_ON_VECTOR_AT = -9.25
+X_NEGATE_AT = (-2.25, -0.25, 3.5, 9.75)
+X_QUANTISE_AFTER = 0.625
 X_BANKS = ((4, 5), (6, 7), (4, 5), (6, 7))
-FAST_COPY = 0
-FINAL_POOL = ()
-ORDER = (0, 1, 6, 4, 2, 8, 9, 3, 7, 22, 21, 23, 24, 27, 28, 25, 29, 26, 11, 33, 34, 30, 5, 97, 13, 78, 31, 77, 98, 32, 14, 36, 58, 57, 10, 38, 100, 37, 40, 80, 39, 109, 12, 110, 117, 60, 118, 15, 44, 43, 41, 112, 42, 48, 45, 46, 49, 47, 120, 16, 50, 66, 68, 65, 67, 70, 69, 72, 51, 73, 71, 74, 17, 126, 53, 18, 61, 125, 64, 52, 55, 19, 56, 150, 54, 113, 75, 62, 149, 81, 20, 128, 114, 82, 76, 102, 161, 35, 90, 162, 63, 106, 101, 86, 121, 152, 79, 133, 87, 105, 84, 91, 134, 88, 122, 111, 173, 154, 164, 104, 153, 174, 92, 165, 136, 59, 83, 185, 186, 89, 85, 103, 176, 166, 99, 198, 94, 177, 130, 93, 188, 197, 127, 95, 115, 129, 178, 210, 116, 209, 137, 200, 138, 119, 190, 96, 124, 221, 189, 132, 123, 212, 131, 233, 222, 202, 201, 234, 213, 277, 214, 224, 140, 139, 236, 225, 107, 226, 237, 108, 238, 291, 155, 141, 156, 167, 142, 168, 179, 146, 157, 309, 144, 191, 180, 143, 169, 192, 145, 181, 158, 148, 193, 170, 284, 249, 203, 159, 299, 204, 147, 182, 215, 251, 171, 160, 298, 292, 183, 252, 285, 175, 194, 135, 151, 278, 205, 286, 172, 227, 279, 217, 239, 323, 245, 206, 216, 310, 184, 255, 246, 163, 195, 223, 196, 253, 229, 281, 247, 316, 228, 241, 311, 248, 280, 187, 256, 240, 293, 282, 287, 324, 259, 218, 199, 289, 330, 257, 294, 208, 300, 207, 230, 211, 331, 220, 263, 219, 254, 242, 346, 301, 261, 345, 296, 231, 317, 332, 283, 260, 288, 318, 243, 312, 325, 295, 356, 232, 368, 319, 235, 357, 302, 305, 290, 258, 326, 347, 244, 297, 306, 303, 367, 348, 358, 304, 349, 307, 359, 308, 350, 333, 265, 378, 360, 351, 369, 361, 362, 267, 371, 271, 370, 268, 372, 264, 379, 313, 389, 269, 373, 320, 390, 380, 270, 314, 272, 266, 327, 275, 321, 384, 273, 334, 400, 382, 391, 383, 274, 276, 315, 401, 381, 250, 338, 328, 394, 337, 262, 322, 393, 411, 412, 392, 339, 352, 402, 329, 335, 340, 363, 395, 342, 403, 422, 374, 341, 406, 385, 413, 336, 404, 423, 396, 343, 353, 415, 414, 424, 407, 405, 344, 417, 425, 416, 426, 435, 354, 364, 433, 436, 428, 365, 437, 434, 427, 439, 375, 438, 418, 441, 376, 440, 386, 443, 355, 442, 387, 445, 397, 444, 366, 447, 398, 446, 408, 429, 448, 377, 419, 449, 388, 430, 451, 450, 409, 399, 453, 452, 420, 410, 455, 454, 431, 421, 456, 457, 432, 459, 458, 461, 460, 463, 462, 464)
+BIAS_LOAD_AT = 2.5
+BIAS_MATMUL_AT = 0.5
+BIAS_COPY_AT = 4.25
+NEXT = 0.001
+ENGINES = ("sync", "scalar", "vector", "tensor")
 
 
 def tile_iwht3layer_pa_kernel(tc, trans, weight, bias, out):
@@ -51,210 +61,230 @@ def tile_iwht3layer_pa_kernel(tc, trans, weight, bias, out):
 
         ident = sbuf.tile([P, P], F32, name="ident")
         ones = sbuf.tile([P, P], BF16, name="ones")
-        bias_pad = sbuf.tile([P, K], BF16, name="bias_pad")
-        bias_sb = sbuf.tile([P, K], F32, name="bias_sb")
-        x_codes = sbuf.tile([P, 4, 1024], U32, name="x_codes", align_bytes=64)
-        x_scales = sbuf.tile([P, 4, 1024], U8, name="x_scales", align_bytes=64)
+        bias_pad = sbuf.tile([P, C_OUT], BF16, name="bias_pad")
+        bias_sb = sbuf.tile([P, C_OUT], F32, name="bias_sb")
+        x_codes = sbuf.tile([P, 4, 8 * P], U32, name="x_codes", align_bytes=64)
+        x_scales = sbuf.tile([P, 4, 8 * P], U8, name="x_scales", align_bytes=64)
         nc.gpsimd.memset(bias_pad[:], 0.0)
         make_identity(nc, ident[:])
         nc.gpsimd.memset(ones[:], 1.0)
         ctx.enter_context(tc.manual_schedule())
 
-        live = {}
-        ops = []
+        program = []
+        tiles = {}
 
-        def tile_of(key, pool, shape, dtype, name):
-            if key not in live:
-                live[key] = pool.tile(shape, dtype, name=name, align_bytes=64) if pool is sbuf else pool.tile(shape, dtype, name=name)
-            return live[key]
+        def op(engine, key, reads, writes, issue):
+            program.append((engine, key, reads, writes, issue))
 
-        def t_xraw(c):
-            return tile_of(("xraw", c), sbuf, [P, 4, C], BF16, "x_raw%d" % c)
+        def tile_of(what, pool, shape, dtype, slot):
+            if what not in tiles:
+                if pool is sbuf:
+                    tiles[what] = pool.tile(shape, dtype, name=slot, align_bytes=64)
+                else:
+                    tiles[what] = pool.tile(shape, dtype, name=slot)
+            return tiles[what]
 
-        def t_xgrp(c):
-            return tile_of(("xgrp", c), sbuf, [P, 2, 4, C], BF16, "x_grp%d" % c)
+        def x_raw(c):
+            return tile_of(("x_raw", c), sbuf, [P, 4, C_IN], BF16, "x_raw%d" % c)
 
-        def t_xt(c, pair):
-            return tile_of(("xt", c, pair), psum, [P, 2, 2, P], F32, "bank%d" % X_BANKS[c][pair])
+        def x_grouped(c):
+            return tile_of(("x_grp", c), sbuf, [P, 2, 4, C_IN], BF16, "x_grp%d" % c)
 
-        def t_raw(s):
-            return tile_of(("raw", s), sbuf, [P, 4, N], BF16, "raw%d" % (s % RAW_BUFS))
+        def x_turned(c, pair):
+            return tile_of(("x_t", c, pair), psum, [P, 2, 2, P], F32, "bank%d" % X_BANKS[c][pair])
 
-        def t_grp(s):
-            return tile_of(("grp", s), sbuf, [P, N, 4], BF16, "grp%d" % (s % GRP_BUFS))
-
-        def t_wc(s):
-            return tile_of(("wc", s), sbuf, [P, N], U32, "w_codes%d" % (s % CODE_BUFS))
-
-        def t_ws(s):
-            return tile_of(("ws", s), sbuf, [P, N], U8, "w_scales%d" % (s % CODE_BUFS))
-
-        def t_acc(h, phase, q, j):
-            return tile_of(("acc", h, phase, q, j), psum, [P, N], F32, "bank%d" % (q + 4 * j))
-
-        def t_part(kind, h, q, a=0, b=0):
-            return tile_of((kind, h, q, a, b), sbuf, [P, N], F32, "%s_%d_%d_%d" % (kind, q, a + 1, b + 1))
-
-        zcount = [0]
-        zslot = {}
-
-        def t_z(h, q, a, b):
-            k = zslot[(h, q, a, b)]
-            return tile_of(("z", h, k // 4), sbuf, [P, 4, N], F32, "x_grp%d" % (k // 4))[:, k % 4, :]
-
-        def op(fn):
-            ops.append(fn)
-
-        def x_chunk(c):
+        def prepare_x(c):
+            quarters = ["x_grp%d.%d" % (c, k) for k in range(4)]
             for pair in range(2):
-                for tt in range(2):
-                    for u in range(2):
-                        op(lambda pair=pair, tt=tt, u=u: nc.tensor.transpose(
-                            t_xt(c, pair)[:, tt, u, :], t_xraw(c)[:].bitcast(F32)[:, 2 * pair + tt, u : C // 2 : 2], ident[:]))
-            for pair in range(2):
-                eng_copy = nc.vector.tensor_copy if (c == 0 and pair == 1) else nc.scalar.copy
-                op(lambda pair=pair, eng_copy=eng_copy: eng_copy(
-                    out=t_xgrp(c)[:, 0, 2 * pair : 2 * pair + 2, :].bitcast(F32).rearrange("p t (r u) -> p t r u", u=2),
-                    in_=t_xt(c, pair)[:].rearrange("p t u r -> p t r u")))
-            op(lambda: nc.vector.tensor_scalar_mul(
-                out=t_xgrp(c)[:, 1, :, :].rearrange("p t k -> p (t k)"),
-                in0=t_xgrp(c)[:, 0, :, :].rearrange("p t k -> p (t k)"), scalar1=-1.0))
-            op(lambda: nc.vector.quantize_mx(
-                out=x_codes[:, c, :].bitcast(MX), scales=x_scales[:, c, :],
-                in_=t_xgrp(c)[:].rearrange("p s t k -> p (s t k)")))
+                bank = "bank%d" % X_BANKS[c][pair]
+                for k in range(2):
+                    for parity in range(2):
+                        op("tensor", X_TURN_AT[c], ["x_raw%d" % c], [bank],
+                           lambda pair=pair, k=k, parity=parity: nc.tensor.transpose(
+                               x_turned(c, pair)[:, k, parity, :],
+                               x_raw(c)[:].bitcast(F32)[:, 2 * pair + k, parity : C_IN // 2 : 2], ident[:]))
+                on_vector = c == 0 and pair == 1
+                op("vector" if on_vector else "scalar", X_COPY_ON_VECTOR_AT if on_vector else X_COPY_AT[c], [bank], [quarters[pair]],
+                   lambda pair=pair, copy=nc.vector.tensor_copy if on_vector else nc.scalar.copy: copy(
+                       out=x_grouped(c)[:, 0, 2 * pair : 2 * pair + 2, :].bitcast(F32).rearrange("p t (m w) -> p t m w", w=2),
+                       in_=x_turned(c, pair)[:].rearrange("p t w m -> p t m w")))
+            op("vector", X_NEGATE_AT[c], quarters[:2], quarters[2:],
+               lambda: nc.vector.tensor_scalar_mul(
+                   out=x_grouped(c)[:, 1, :, :].rearrange("p t k -> p (t k)"),
+                   in0=x_grouped(c)[:, 0, :, :].rearrange("p t k -> p (t k)"), scalar1=-1.0))
+            op("vector", X_NEGATE_AT[c] + X_QUANTISE_AFTER, quarters, ["x_codes%d" % c],
+               lambda: nc.vector.quantize_mx(
+                   out=x_codes[:, c, :].bitcast(E5M2_X4), scales=x_scales[:, c, :],
+                   in_=x_grouped(c)[:].rearrange("p s t k -> p (s t k)")))
 
         def x_operand(t, sign):
-            lo = (0 if sign > 0 else 512) + (t % 4) * P
-            return x_codes[:, t // 4, lo : lo + P].bitcast(MX), x_scales[:, t // 4, lo : lo + P]
+            first = (0 if sign > 0 else 4 * P) + (t % 4) * P
+            return x_codes[:, t // 4, first : first + P].bitcast(E5M2_X4), x_scales[:, t // 4, first : first + P]
 
-        def bias_to_all():
+        def spread_bias():
             for h in range(HALVES):
-                key = ("pb", h)
-                op(lambda h=h, key=key: nc.tensor.matmul(
-                    out=tile_of(key, psum, [P, N], F32, "bank%d" % (6 + h))[:], lhsT=ones[:],
-                    rhs=bias_pad[:, h * N : (h + 1) * N], start=True, stop=True))
-                op(lambda h=h, key=key: nc.scalar.copy(out=bias_sb[:, h * N : (h + 1) * N], in_=live[key][:]))
+                bank = "bank%d" % (6 + h)
+                cols = slice(h * N, (h + 1) * N)
+                op("tensor", BIAS_MATMUL_AT, ["bias_pad"], [bank],
+                   lambda h=h, bank=bank, cols=cols: nc.tensor.matmul(
+                       out=tile_of(("bias", h), psum, [P, N], F32, bank)[:], lhsT=ones[:], rhs=bias_pad[:, cols],
+                       start=True, stop=True))
+                op("scalar", BIAS_COPY_AT, [bank], ["bias_sb%d" % h],
+                   lambda h=h, cols=cols: nc.scalar.copy(out=bias_sb[:, cols], in_=tiles[("bias", h)][:]))
+
+        def w_raw(s):
+            return tile_of(("raw", s), sbuf, [P, 4, N], BF16, "raw%d" % (s % RAW_SLOTS))
+
+        def w_grouped(s):
+            return tile_of(("grp", s), sbuf, [P, N, 4], BF16, "grp%d" % (s % GROUPED_SLOTS))
+
+        def w_codes(s):
+            return tile_of(("wc", s), sbuf, [P, N], U32, "w_codes%d" % (s % CODE_SLOTS))
+
+        def w_scales(s):
+            return tile_of(("ws", s), sbuf, [P, N], U8, "w_scales%d" % (s % CODE_SLOTS))
 
         def load_w(s):
             h, t = divmod(s, COEFFS)
-            op(lambda: nc.sync.dma_start(out=t_raw(s)[:], in_=w_view[t, :, :, h * N : (h + 1) * N]))
+            op("sync", s, [], ["raw%d" % (s % RAW_SLOTS)],
+               lambda: nc.sync.dma_start(out=w_raw(s)[:], in_=w_view[t, :, :, h * N : (h + 1) * N]))
 
-        def views(s, lo, hi):
-            if FAST_COPY:
-                return (t_grp(s)[:, lo:hi, :].rearrange("p (c i) r -> p c r i", i=4),
-                        t_raw(s)[:, :, lo:hi].rearrange("p r (c i) -> p c r i", i=4))
-            return t_grp(s)[:, lo:hi, :], t_raw(s)[:, :, lo:hi].rearrange("p r n -> p n r")
+        def interleave(copy, s):
+            copy(out=w_grouped(s)[:], in_=w_raw(s)[:].rearrange("p r n -> p n r"))
 
-        def s_part(s, lo, hi):
-            dst, src = views(s, lo, hi)
-            nc.scalar.copy(out=dst, in_=src)
+        def quantise_at(s):
+            return s - AHEAD[s // 4]
 
-        def v_part(s, lo, hi):
-            dst, src = views(s, lo, hi)
-            nc.vector.tensor_copy(out=dst, in_=src)
-
-        def g_part(s, lo, hi):
-            nc.gpsimd.tensor_scalar(out=t_grp(s)[:, lo:hi, :], in0=t_raw(s)[:, :, lo:hi].rearrange("p r n -> p n r"),
-                                    scalar1=1.0, scalar2=0.0, op0=MULT, op1=ADD)
-
-        def produce(s):
-            a = S_COLS[s]
-            b = N - G_COLS[s]
-            if a > 0:
-                op(lambda: s_part(s, 0, a))
-            if b > a:
-                op(lambda: v_part(s, a, b))
-            if b < N:
-                op(lambda: g_part(s, b, N))
-            if s + RAW_BUFS < STEPS:
-                load_w(s + RAW_BUFS)
-            op(lambda: nc.vector.quantize_mx(out=t_wc(s)[:].bitcast(MX), scales=t_ws(s)[:],
-                                             in_=t_grp(s)[:].rearrange("p n r -> p (n r)")))
-
-        def combine(dst, src, factor, sb):
-            nc.vector.scalar_tensor_tensor(out=dst, in0=src[:], scalar=factor, in1=sb, op0=MULT, op1=ADD)
-
-        def store(h, q, a, b):
-            zslot[(h, q, a, b)] = zcount[0] % 16
-            zcount[0] += 1
-            p = (0 if a > 0 else 1) + (0 if b > 0 else 2)
-            op(lambda: nc.sync.dma_start(out=out_view[p, q, :, :, h * N : (h + 1) * N], in_=t_z(h, q, a, b)))
-
-        def closed(h, phase, q, j, form):
-            a = 1 if j == 0 else -1
-            cols = slice(h * N, (h + 1) * N)
-            src = lambda: t_acc(h, phase, q, j)
-            if phase == 0:
-                if form == "pe":
-                    op(lambda: combine(t_part("s", h, q, a)[:], src(), 1.0 / 16, bias_sb[:, cols]))
-                elif j == 0:
-                    op(lambda: combine(t_part("base", h, q)[:], src(), 1.0 / 16, bias_sb[:, cols]))
-                else:
-                    for aa in (1, -1):
-                        op(lambda aa=aa: combine(t_part("s", h, q, aa)[:], src(), aa / 16.0, t_part("base", h, q)[:]))
-            elif form == "pe":
-                if h == HALVES - 1 and (q + 4 * j) in FINAL_POOL:
-                    op(lambda: nc.scalar.mul(out=t_part("t", h, q, a)[:], in_=src()[:], mul=1.0 / 16))
-                    for bb in (1, -1):
-                        op(lambda bb=bb: nc.gpsimd.tensor_tensor(out=t_z(h, q, a, bb), in0=t_part("s", h, q, a)[:],
-                                                                 in1=t_part("t", h, q, a)[:], op=ADD if bb > 0 else SUB))
-                        store(h, q, a, bb)
-                else:
-                    for bb in (1, -1):
-                        op(lambda bb=bb: combine(t_z(h, q, a, bb), src(), bb / 16.0, t_part("s", h, q, a)[:]))
-                        store(h, q, a, bb)
-            elif j == 0:
-                for aa in (1, -1):
-                    for bb in (1, -1):
-                        op(lambda aa=aa, bb=bb: combine(t_part("w", h, q, aa, bb)[:], src(), bb / 16.0, t_part("s", h, q, aa)[:]))
+        def prepare_w(s):
+            raw = "raw%d" % (s % RAW_SLOTS)
+            grouped = "grp%d" % (s % GROUPED_SLOTS)
+            if s in VECTOR_TILES:
+                op("vector", quantise_at(s) - COPY_BEFORE, [raw], [grouped], lambda: interleave(nc.vector.tensor_copy, s))
             else:
-                for aa in (1, -1):
-                    for bb in (1, -1):
-                        op(lambda aa=aa, bb=bb: combine(t_z(h, q, aa, bb), src(), aa * bb / 16.0, t_part("w", h, q, aa, bb)[:]))
-                        store(h, q, aa, bb)
+                op("scalar", s, [raw], [grouped], lambda: interleave(nc.scalar.copy, s))
+            if s + RAW_SLOTS < TILES:
+                load_w(s + RAW_SLOTS)
+            op("vector", quantise_at(s), [grouped], ["codes%d" % (s % CODE_SLOTS)],
+               lambda: nc.vector.quantize_mx(
+                   out=w_codes(s)[:].bitcast(E5M2_X4), scales=w_scales(s)[:],
+                   in_=w_grouped(s)[:].rearrange("p n r -> p (n r)")))
+
+        def group(h, phase, q, j):
+            return tile_of(("acc", h, phase, q, j), psum, [P, N], F32, "bank%d" % (q + 4 * j))
+
+        def base_slot(q):
+            return "base%d" % q
+
+        def s_slot(q, a):
+            return "s%d_%s" % (q, "plus" if a > 0 else "minus")
+
+        def base(h, q):
+            return tile_of(("base", h, q), sbuf, [P, N], F32, base_slot(q))
+
+        def s_sum(h, q, a):
+            return tile_of(("s", h, q, a), sbuf, [P, N], F32, s_slot(q, a))
+
+        place_of = {}
+
+        def result(h, q, a, b):
+            k = place_of[(h, q, a, b)]
+            return tile_of(("z", h, k // 4), sbuf, [P, 4, N], F32, "x_grp%d" % (k // 4))[:, k % 4, :]
+
+        def scaled_sum(dst, h, phase, q, j, factor, addend):
+            nc.vector.scalar_tensor_tensor(out=dst, in0=group(h, phase, q, j)[:], scalar=factor, in1=addend,
+                                           op0=MULT, op1=ADD)
+
+        def sums_of(h, phase, q, j):
+            bank = "bank%d" % (q + 4 * j)
+            done = COEFFS * h + (15 if phase == 1 else 3 + 4 * j) + LAG[h][phase][j][q]
+            if phase == 0 and j == 0:
+                op("vector", done + SUM_AFTER[0], [bank, "bias_sb%d" % h], [base_slot(q)],
+                   lambda: scaled_sum(base(h, q)[:], h, 0, q, 0, 1.0 / 16, bias_sb[:, h * N : (h + 1) * N]))
+            elif phase == 0:
+                for a in (1, -1):
+                    op("vector", done + SUM_AFTER[1] + (NEXT if a < 0 else 0.0), [bank, base_slot(q)], [s_slot(q, a)],
+                       lambda a=a: scaled_sum(s_sum(h, q, a)[:], h, 0, q, 1, a / 16.0, base(h, q)[:]))
+            else:
+                a = 1 if j == 0 else -1
+                for b in (1, -1):
+                    at = done + SUM_AFTER[2] + (NEXT if b < 0 else 0.0)
+                    k = len(place_of) % 16
+                    place_of[(h, q, a, b)] = k
+                    place = "x_grp%d.%d" % (k // 4, k % 4)
+                    row = (0 if a > 0 else 1) + (0 if b > 0 else 2)
+                    op("vector", at, [bank, s_slot(q, a)], [place],
+                       lambda b=b: scaled_sum(result(h, q, a, b), h, 1, q, j, b / 16.0, s_sum(h, q, a)[:]))
+                    op("sync", 100.0 + at, [place], [],
+                       lambda b=b, row=row: nc.sync.dma_start(out=out_view[row, q, :, :, h * N : (h + 1) * N],
+                                                              in_=result(h, q, a, b)))
 
         def one_pass(s, q, j, sign, start, stop):
             h, t = divmod(s, COEFFS)
             lhsT, lhsT_scale = x_operand(t, sign)
-            nc.tensor.matmul_mx(out=t_acc(h, t // 8, q, j)[:], lhsT=lhsT, lhsT_scale=lhsT_scale,
-                                rhs=t_wc(s)[:].bitcast(MX), rhs_scale=t_ws(s)[:], start=start, stop=stop)
+            nc.tensor.matmul_mx(out=group(h, t // 8, q, j)[:], lhsT=lhsT, lhsT_scale=lhsT_scale,
+                                rhs=w_codes(s)[:].bitcast(E5M2_X4), rhs_scale=w_scales(s)[:], start=start, stop=stop)
 
-        def passes(s):
+        def multiply(s):
             h, t = divmod(s, COEFFS)
             u, v = divmod(t, 4)
-            phase, uu = divmod(u, 2)
-            ends = []
+            phase = u // 2
+            ended = []
             for j in range(2):
                 for q in range(4):
-                    form = (FORM1 if phase == 0 else FORM2)[h][q]
-                    if form == "pe":
-                        sign = HAD[q][v] * (-1 if (j == 1 and uu == 1) else 1)
-                        start, stop = uu == 0 and v == 0, uu == 1 and v == 3
-                    elif j == uu:
-                        sign, start, stop = HAD[q][v], v == 0, v == 3
-                    else:
+                    if phase == 0 and j != u:
                         continue
-                    op(lambda q=q, j=j, sign=sign, start=start, stop=stop: one_pass(s, q, j, sign, start, stop))
+                    sign = HAD[q][v] * (-1 if (phase == 1 and j == 1 and u == 3) else 1)
+                    start = v == 0 and u != 3
+                    stop = v == 3 and u != 2
+                    op("tensor", s + LAG[h][phase][j][q] + NEXT * (4 * j + q),
+                       ["codes%d" % (s % CODE_SLOTS), "x_codes%d" % (t // 4)], ["bank%d" % (q + 4 * j)],
+                       lambda q=q, j=j, sign=sign, start=start, stop=stop: one_pass(s, q, j, sign, start, stop))
                     if stop:
-                        ends.append((h, phase, q, j, form))
-            for e in ends:
-                closed(e[0], e[1], e[2], e[3], e[4])
+                        ended.append((q, j))
+            for q, j in ended:
+                sums_of(h, phase, q, j)
 
-        for item in list(LOADS) + list(range(6, RAW_BUFS)):
-            if item == "b":
-                op(lambda: nc.sync.dma_start(out=bias_pad[0:1, :], in_=bias_row))
-            elif isinstance(item, str):
-                op(lambda c=int(item[1]): nc.sync.dma_start(out=t_xraw(c)[:], in_=x_view[:, 4 * c : 4 * c + 4, :]))
-            else:
-                load_w(item)
-        for s in range(STEPS):
-            for c in range(4):
-                if X_AT[c] == s:
-                    x_chunk(c)
-                    if c == 1:
-                        bias_to_all()
-            produce(s)
-            passes(s)
+        for c in range(4):
+            op("sync", X_LOAD_AT[c], [], ["x_raw%d" % c],
+               lambda c=c: nc.sync.dma_start(out=x_raw(c)[:], in_=x_view[:, 4 * c : 4 * c + 4, :]))
+        op("sync", BIAS_LOAD_AT, [], ["bias_pad"], lambda: nc.sync.dma_start(out=bias_pad[0:1, :], in_=bias_row))
+        for s in range(RAW_SLOTS):
+            load_w(s)
+        for s in range(TILES):
+            if s < 4:
+                prepare_x(s)
+            if s == 1:
+                spread_bias()
+            prepare_w(s)
+            multiply(s)
 
-        for k in (ORDER if ORDER else range(len(ops))):
-            ops[k]()
+        behind = []
+        writer = {}
+        readers = {}
+        for n, entry in enumerate(program):
+            need = set()
+            for slot in entry[2]:
+                if slot in writer:
+                    need.add(writer[slot])
+                readers.setdefault(slot, []).append(n)
+            for slot in entry[3]:
+                if slot in writer:
+                    need.add(writer[slot])
+                for m in readers.get(slot, []):
+                    if m != n:
+                        need.add(m)
+                writer[slot] = n
+                readers[slot] = []
+            behind.append(need)
+
+        queues = {e: sorted([n for n in range(len(program)) if program[n][0] == e], key=lambda n: (program[n][1], n))
+                  for e in ENGINES}
+        issued = set()
+        while len(issued) < len(program):
+            before = len(issued)
+            for e in ENGINES:
+                while queues[e] and behind[queues[e][0]] <= issued:
+                    n = queues[e].pop(0)
+                    program[n][4]()
+                    issued.add(n)
+            assert len(issued) > before, "the engines' orders contradict the dataflow"

@@ -7,45 +7,37 @@ F32 = mybir.dt.float32
 BF16 = mybir.dt.bfloat16
 U32 = mybir.dt.uint32
 U8 = mybir.dt.uint8
-E5M2_X4 = mybir.dt.float8_e5m2_x4
+MX = mybir.dt.float8_e5m2_x4
 MULT = mybir.AluOpType.mult
 ADD = mybir.AluOpType.add
 
 P = 128
 COEFFS = 16
-C_IN = 512
-C_OUT = 1024
+C = 512
+K = 1024
 N = 512
-HALVES = C_OUT // N
-TILES = COEFFS * HALVES
+HALVES = K // N
+PANELS = COEFFS * HALVES
 HAD = ((1, 1, 1, 1), (1, -1, 1, -1), (1, 1, -1, -1), (1, -1, -1, 1))
-FLOPS = 2 * COEFFS * P * C_IN * C_OUT
+FLOPS = 2 * COEFFS * P * C * K
 
-RAW_SLOTS = 16
-GROUPED_SLOTS = 5
-CODE_SLOTS = 10
-
-VECTOR_TILES = (1, 4, 6, 9, 12, 16, 17, 25, 28)
-
-LAG = (
-    (((-2.0, 0.75, 0.5, 0.0), (-1.5, -0.75, 2.0, 1.5)), ((-1.75, -1.5, -1.5, -2.0), (0.25, 1.0, 3.75, 3.25))),
-    (((1.0, 2.5, 2.5, 2.25), (1.0, -0.5, 4.0, 2.0)), ((1.25, 1.5, 1.5, 1.25), (7.0, 5.25, 11.25, 13.75))),
-)
-AHEAD = (2.5, 2.75, 1.25, 1.75, 2.0, 2.25, 2.75, 3.25)
-COPY_BEFORE = 1.5
-SUM_AFTER = (0.75, 2.25, 2.25)
-X_LOAD_AT = (-5.5, 2.75, 6.0, 10.0)
-X_TURN_AT = (-11.75, -6.5, 1.75, 4.25)
-X_COPY_AT = (-5.0, 2.5, 6.0, 8.25)
-X_COPY_ON_VECTOR_AT = -9.25
-X_NEGATE_AT = (-2.25, -0.25, 3.5, 9.75)
-X_QUANTISE_AFTER = 0.625
+RAW_BUFS = 16
+GRP_BUFS = 3
+CODE_BUFS = 10
+LEAD = 2
+V_EPI = 2
+PE_BUDGET = 5
+E_LAG = 0
+QMAJOR = 1
+SPLIT = ((320, 0), (320, 96), (352, 160))
+RANK = {"T+": 0, "T-": 1, "r0": 2, "r1": 2}
+SEQ_HEAD = ("x0", 0, "x1", 1, "x2", 2, "x3", 3, "b")
+LEAD_T = 4
+LOADS_AHEAD = 16
+EARLY = 8
+SPLIT_EARLY = (352, 0)
 X_BANKS = ((4, 5), (6, 7), (4, 5), (6, 7))
-BIAS_LOAD_AT = 2.5
-BIAS_MATMUL_AT = 0.5
-BIAS_COPY_AT = 4.25
-NEXT = 0.001
-ENGINES = ("sync", "scalar", "vector", "tensor")
+BIAS_BANKS = (4, 5)
 
 
 def tile_iwht3layer_pa_kernel(tc, trans, weight, bias, out):
@@ -61,230 +53,227 @@ def tile_iwht3layer_pa_kernel(tc, trans, weight, bias, out):
 
         ident = sbuf.tile([P, P], F32, name="ident")
         ones = sbuf.tile([P, P], BF16, name="ones")
-        bias_pad = sbuf.tile([P, C_OUT], BF16, name="bias_pad")
-        bias_sb = sbuf.tile([P, C_OUT], F32, name="bias_sb")
-        x_codes = sbuf.tile([P, 4, 8 * P], U32, name="x_codes", align_bytes=64)
-        x_scales = sbuf.tile([P, 4, 8 * P], U8, name="x_scales", align_bytes=64)
-        nc.gpsimd.memset(bias_pad[:], 0.0)
+        bias_pad = sbuf.tile([P, K], BF16, name="bias_pad")
+        bias_sb = sbuf.tile([P, K], F32, name="bias_sb")
+        x_codes = sbuf.tile([P, 4, 1024], U32, name="x_codes", align_bytes=64)
+        x_scales = sbuf.tile([P, 4, 1024], U8, name="x_scales", align_bytes=64)
         make_identity(nc, ident[:])
+        nc.gpsimd.memset(bias_pad[:], 0.0)
         nc.gpsimd.memset(ones[:], 1.0)
         ctx.enter_context(tc.manual_schedule())
 
-        program = []
-        tiles = {}
+        raw, grp, wc, ws, x_raw, x_grp = {}, {}, {}, {}, {}, {}
+        bank_busy = [False] * 8
 
-        def op(engine, key, reads, writes, issue):
-            program.append((engine, key, reads, writes, issue))
+        def sb(tag, shape, dtype):
+            return sbuf.tile(shape, dtype, name=tag, align_bytes=64)
 
-        def tile_of(what, pool, shape, dtype, slot):
-            if what not in tiles:
-                if pool is sbuf:
-                    tiles[what] = pool.tile(shape, dtype, name=slot, align_bytes=64)
-                else:
-                    tiles[what] = pool.tile(shape, dtype, name=slot)
-            return tiles[what]
+        def bank(b, shape):
+            return psum.tile(shape, F32, name="bank%d" % b)
 
-        def x_raw(c):
-            return tile_of(("x_raw", c), sbuf, [P, 4, C_IN], BF16, "x_raw%d" % c)
+        def load_x(c):
+            x_raw[c] = sb("x_raw%d" % c, [P, 4, C], BF16)
+            nc.sync.dma_start(out=x_raw[c][:], in_=x_view[:, 4 * c : 4 * c + 4, :])
 
-        def x_grouped(c):
-            return tile_of(("x_grp", c), sbuf, [P, 2, 4, C_IN], BF16, "x_grp%d" % c)
-
-        def x_turned(c, pair):
-            return tile_of(("x_t", c, pair), psum, [P, 2, 2, P], F32, "bank%d" % X_BANKS[c][pair])
-
-        def prepare_x(c):
-            quarters = ["x_grp%d.%d" % (c, k) for k in range(4)]
-            for pair in range(2):
-                bank = "bank%d" % X_BANKS[c][pair]
-                for k in range(2):
-                    for parity in range(2):
-                        op("tensor", X_TURN_AT[c], ["x_raw%d" % c], [bank],
-                           lambda pair=pair, k=k, parity=parity: nc.tensor.transpose(
-                               x_turned(c, pair)[:, k, parity, :],
-                               x_raw(c)[:].bitcast(F32)[:, 2 * pair + k, parity : C_IN // 2 : 2], ident[:]))
-                on_vector = c == 0 and pair == 1
-                op("vector" if on_vector else "scalar", X_COPY_ON_VECTOR_AT if on_vector else X_COPY_AT[c], [bank], [quarters[pair]],
-                   lambda pair=pair, copy=nc.vector.tensor_copy if on_vector else nc.scalar.copy: copy(
-                       out=x_grouped(c)[:, 0, 2 * pair : 2 * pair + 2, :].bitcast(F32).rearrange("p t (m w) -> p t m w", w=2),
-                       in_=x_turned(c, pair)[:].rearrange("p t w m -> p t m w")))
-            op("vector", X_NEGATE_AT[c], quarters[:2], quarters[2:],
-               lambda: nc.vector.tensor_scalar_mul(
-                   out=x_grouped(c)[:, 1, :, :].rearrange("p t k -> p (t k)"),
-                   in0=x_grouped(c)[:, 0, :, :].rearrange("p t k -> p (t k)"), scalar1=-1.0))
-            op("vector", X_NEGATE_AT[c] + X_QUANTISE_AFTER, quarters, ["x_codes%d" % c],
-               lambda: nc.vector.quantize_mx(
-                   out=x_codes[:, c, :].bitcast(E5M2_X4), scales=x_scales[:, c, :],
-                   in_=x_grouped(c)[:].rearrange("p s t k -> p (s t k)")))
-
-        def x_operand(t, sign):
-            first = (0 if sign > 0 else 4 * P) + (t % 4) * P
-            return x_codes[:, t // 4, first : first + P].bitcast(E5M2_X4), x_scales[:, t // 4, first : first + P]
-
-        def spread_bias():
-            for h in range(HALVES):
-                bank = "bank%d" % (6 + h)
-                cols = slice(h * N, (h + 1) * N)
-                op("tensor", BIAS_MATMUL_AT, ["bias_pad"], [bank],
-                   lambda h=h, bank=bank, cols=cols: nc.tensor.matmul(
-                       out=tile_of(("bias", h), psum, [P, N], F32, bank)[:], lhsT=ones[:], rhs=bias_pad[:, cols],
-                       start=True, stop=True))
-                op("scalar", BIAS_COPY_AT, [bank], ["bias_sb%d" % h],
-                   lambda h=h, cols=cols: nc.scalar.copy(out=bias_sb[:, cols], in_=tiles[("bias", h)][:]))
-
-        def w_raw(s):
-            return tile_of(("raw", s), sbuf, [P, 4, N], BF16, "raw%d" % (s % RAW_SLOTS))
-
-        def w_grouped(s):
-            return tile_of(("grp", s), sbuf, [P, N, 4], BF16, "grp%d" % (s % GROUPED_SLOTS))
-
-        def w_codes(s):
-            return tile_of(("wc", s), sbuf, [P, N], U32, "w_codes%d" % (s % CODE_SLOTS))
-
-        def w_scales(s):
-            return tile_of(("ws", s), sbuf, [P, N], U8, "w_scales%d" % (s % CODE_SLOTS))
+        def load(item):
+            if item == "b":
+                nc.sync.dma_start(out=bias_pad[0:1, :], in_=bias_row)
+            elif isinstance(item, str):
+                load_x(int(item[1]))
+            else:
+                load_w(item)
 
         def load_w(s):
             h, t = divmod(s, COEFFS)
-            op("sync", s, [], ["raw%d" % (s % RAW_SLOTS)],
-               lambda: nc.sync.dma_start(out=w_raw(s)[:], in_=w_view[t, :, :, h * N : (h + 1) * N]))
+            raw[s] = sb("raw%d" % (s % RAW_BUFS), [P, 4, N], BF16)
+            nc.sync.dma_start(out=raw[s][:], in_=w_view[t, :, :, h * N : (h + 1) * N])
 
-        def interleave(copy, s):
-            copy(out=w_grouped(s)[:], in_=w_raw(s)[:].rearrange("p r n -> p n r"))
+        turned = {}
 
-        def quantise_at(s):
-            return s - AHEAD[s // 4]
+        def x_turn(c):
+            words = x_raw[c][:].bitcast(F32)
+            for pair in range(2):
+                assert not bank_busy[X_BANKS[c][pair]]
+                xt = bank(X_BANKS[c][pair], [P, 2, 2, P])
+                turned[c, pair] = xt
+                for tt in range(2):
+                    for u in range(2):
+                        nc.tensor.transpose(xt[:, tt, u, :], words[:, 2 * pair + tt, u : C // 2 : 2], ident[:])
 
-        def prepare_w(s):
-            raw = "raw%d" % (s % RAW_SLOTS)
-            grouped = "grp%d" % (s % GROUPED_SLOTS)
-            if s in VECTOR_TILES:
-                op("vector", quantise_at(s) - COPY_BEFORE, [raw], [grouped], lambda: interleave(nc.vector.tensor_copy, s))
-            else:
-                op("scalar", s, [raw], [grouped], lambda: interleave(nc.scalar.copy, s))
-            if s + RAW_SLOTS < TILES:
-                load_w(s + RAW_SLOTS)
-            op("vector", quantise_at(s), [grouped], ["codes%d" % (s % CODE_SLOTS)],
-               lambda: nc.vector.quantize_mx(
-                   out=w_codes(s)[:].bitcast(E5M2_X4), scales=w_scales(s)[:],
-                   in_=w_grouped(s)[:].rearrange("p n r -> p (n r)")))
+        def x_copy(c, first):
+            x_grp[c] = sb("x_grp%d" % c, [P, 2, 4, C], BF16)
+            for pair in range(2):
+                copy = nc.vector.tensor_copy if (first and pair == 1) else nc.scalar.copy
+                copy(out=x_grp[c][:, 0, 2 * pair : 2 * pair + 2, :].bitcast(F32).rearrange("p t (r u) -> p t r u", u=2),
+                     in_=turned[c, pair][:].rearrange("p t u r -> p t r u"))
 
-        def group(h, phase, q, j):
-            return tile_of(("acc", h, phase, q, j), psum, [P, N], F32, "bank%d" % (q + 4 * j))
+        def x_quant(c, sign):
+            nc.vector.quantize_mx(out=x_codes[:, c, 512 * sign : 512 * sign + 512].bitcast(MX),
+                                  scales=x_scales[:, c, 512 * sign : 512 * sign + 512],
+                                  in_=x_grp[c][:, sign, :, :].rearrange("p t k -> p (t k)"))
 
-        def base_slot(q):
-            return "base%d" % q
+        def x_negate(c):
+            nc.vector.tensor_scalar_mul(out=x_grp[c][:, 1, :, :].rearrange("p t k -> p (t k)"),
+                                        in0=x_grp[c][:, 0, :, :].rearrange("p t k -> p (t k)"), scalar1=-1.0)
 
-        def s_slot(q, a):
-            return "s%d_%s" % (q, "plus" if a > 0 else "minus")
+        def bias_mm():
+            for h in range(HALVES):
+                assert not bank_busy[BIAS_BANKS[h]]
+                turned["b", h] = bank(BIAS_BANKS[h], [P, N])
+                nc.tensor.matmul(out=turned["b", h][:], lhsT=ones[:], rhs=bias_pad[:, h * N : (h + 1) * N], start=True, stop=True)
 
-        def base(h, q):
-            return tile_of(("base", h, q), sbuf, [P, N], F32, base_slot(q))
+        def bias_copy():
+            for h in range(HALVES):
+                nc.scalar.copy(out=bias_sb[:, h * N : (h + 1) * N], in_=turned["b", h][:])
 
-        def s_sum(h, q, a):
-            return tile_of(("s", h, q, a), sbuf, [P, N], F32, s_slot(q, a))
+        def interleave(s, s_cols, g_cols):
+            grp[s] = sb("grp%d" % (s % GRP_BUFS), [P, N, 4], BF16)
+            cuts = (0, s_cols, s_cols + g_cols, N)
+            for e in range(3):
+                lo, hi = cuts[e], cuts[e + 1]
+                if hi == lo:
+                    continue
+                dst, src = grp[s][:, lo:hi, :], raw[s][:, :, lo:hi].rearrange("p r n -> p n r")
+                if e == 0:
+                    nc.scalar.copy(out=dst, in_=src)
+                elif e == 1:
+                    nc.gpsimd.tensor_scalar(out=dst, in0=src, scalar1=1.0, scalar2=0.0, op0=MULT, op1=ADD)
+                else:
+                    nc.vector.tensor_copy(out=dst, in_=src)
 
-        place_of = {}
+        def quantise(s):
+            wc[s] = sb("w_codes%d" % (s % CODE_BUFS), [P, N], U32)
+            ws[s] = sb("w_scales%d" % (s % CODE_BUFS), [P, N], U8)
+            nc.vector.quantize_mx(out=wc[s][:].bitcast(MX), scales=ws[s][:], in_=grp[s][:].rearrange("p n r -> p (n r)"))
 
-        def result(h, q, a, b):
-            k = place_of[(h, q, a, b)]
-            return tile_of(("z", h, k // 4), sbuf, [P, 4, N], F32, "x_grp%d" % (k // 4))[:, k % 4, :]
-
-        def scaled_sum(dst, h, phase, q, j, factor, addend):
-            nc.vector.scalar_tensor_tensor(out=dst, in0=group(h, phase, q, j)[:], scalar=factor, in1=addend,
-                                           op0=MULT, op1=ADD)
-
-        def sums_of(h, phase, q, j):
-            bank = "bank%d" % (q + 4 * j)
-            done = COEFFS * h + (15 if phase == 1 else 3 + 4 * j) + LAG[h][phase][j][q]
-            if phase == 0 and j == 0:
-                op("vector", done + SUM_AFTER[0], [bank, "bias_sb%d" % h], [base_slot(q)],
-                   lambda: scaled_sum(base(h, q)[:], h, 0, q, 0, 1.0 / 16, bias_sb[:, h * N : (h + 1) * N]))
-            elif phase == 0:
-                for a in (1, -1):
-                    op("vector", done + SUM_AFTER[1] + (NEXT if a < 0 else 0.0), [bank, base_slot(q)], [s_slot(q, a)],
-                       lambda a=a: scaled_sum(s_sum(h, q, a)[:], h, 0, q, 1, a / 16.0, base(h, q)[:]))
-            else:
-                a = 1 if j == 0 else -1
-                for b in (1, -1):
-                    at = done + SUM_AFTER[2] + (NEXT if b < 0 else 0.0)
-                    k = len(place_of) % 16
-                    place_of[(h, q, a, b)] = k
-                    place = "x_grp%d.%d" % (k // 4, k % 4)
-                    row = (0 if a > 0 else 1) + (0 if b > 0 else 2)
-                    op("vector", at, [bank, s_slot(q, a)], [place],
-                       lambda b=b: scaled_sum(result(h, q, a, b), h, 1, q, j, b / 16.0, s_sum(h, q, a)[:]))
-                    op("sync", 100.0 + at, [place], [],
-                       lambda b=b, row=row: nc.sync.dma_start(out=out_view[row, q, :, :, h * N : (h + 1) * N],
-                                                              in_=result(h, q, a, b)))
-
-        def one_pass(s, q, j, sign, start, stop):
-            h, t = divmod(s, COEFFS)
-            lhsT, lhsT_scale = x_operand(t, sign)
-            nc.tensor.matmul_mx(out=group(h, t // 8, q, j)[:], lhsT=lhsT, lhsT_scale=lhsT_scale,
-                                rhs=w_codes(s)[:].bitcast(E5M2_X4), rhs_scale=w_scales(s)[:], start=start, stop=stop)
-
-        def multiply(s):
-            h, t = divmod(s, COEFFS)
-            u, v = divmod(t, 4)
-            phase = u // 2
-            ended = []
-            for j in range(2):
+        groups = []
+        for h in range(HALVES):
+            for kind, first, count, b0 in (("r0", 0, 4, 0), ("r1", 4, 4, 4), ("T+", 8, 8, 0), ("T-", 8, 8, 4)):
                 for q in range(4):
-                    if phase == 0 and j != u:
-                        continue
-                    sign = HAD[q][v] * (-1 if (phase == 1 and j == 1 and u == 3) else 1)
-                    start = v == 0 and u != 3
-                    stop = v == 3 and u != 2
-                    op("tensor", s + LAG[h][phase][j][q] + NEXT * (4 * j + q),
-                       ["codes%d" % (s % CODE_SLOTS), "x_codes%d" % (t // 4)], ["bank%d" % (q + 4 * j)],
-                       lambda q=q, j=j, sign=sign, start=start, stop=stop: one_pass(s, q, j, sign, start, stop))
-                    if stop:
-                        ended.append((q, j))
-            for q, j in ended:
-                sums_of(h, phase, q, j)
+                    groups.append({"kind": kind, "h": h, "q": q, "bank": b0 + q, "panels": [COEFFS * h + first + i for i in range(count)],
+                                   "at": 0, "tile": None})
+        used = [0] * PANELS
+        pending = []
+        part = {}
+        z_count = [0]
+        z_tiles = {}
 
-        for c in range(4):
-            op("sync", X_LOAD_AT[c], [], ["x_raw%d" % c],
-               lambda c=c: nc.sync.dma_start(out=x_raw(c)[:], in_=x_view[:, 4 * c : 4 * c + 4, :]))
-        op("sync", BIAS_LOAD_AT, [], ["bias_pad"], lambda: nc.sync.dma_start(out=bias_pad[0:1, :], in_=bias_row))
-        for s in range(RAW_SLOTS):
-            load_w(s)
-        for s in range(TILES):
-            if s < 4:
-                prepare_x(s)
-            if s == 1:
-                spread_bias()
-            prepare_w(s)
-            multiply(s)
+        def one_pass(g):
+            s = g["panels"][g["at"]]
+            t = s % COEFFS
+            u, v = divmod(t, 4)
+            sign = HAD[g["q"]][v] * (-1 if (g["kind"] == "T-" and u == 3) else 1)
+            lo = (0 if sign > 0 else 512) + (t % 4) * P
+            nc.tensor.matmul_mx(out=g["tile"][:], lhsT=x_codes[:, t // 4, lo : lo + P].bitcast(MX), lhsT_scale=x_scales[:, t // 4, lo : lo + P],
+                                rhs=wc[s][:].bitcast(MX), rhs_scale=ws[s][:], start=g["at"] == 0, stop=g["at"] == len(g["panels"]) - 1)
+            g["at"] += 1
+            used[s] += 1
 
-        behind = []
-        writer = {}
-        readers = {}
-        for n, entry in enumerate(program):
-            need = set()
-            for slot in entry[2]:
-                if slot in writer:
-                    need.add(writer[slot])
-                readers.setdefault(slot, []).append(n)
-            for slot in entry[3]:
-                if slot in writer:
-                    need.add(writer[slot])
-                for m in readers.get(slot, []):
-                    if m != n:
-                        need.add(m)
-                writer[slot] = n
-                readers[slot] = []
-            behind.append(need)
+        def pe_step(done, step, last, extra):
+            left = 1000 if last else PE_BUDGET + extra
+            while left > 0:
+                ready = [g for g in groups if g["at"] < len(g["panels"]) and g["panels"][g["at"]] <= done
+                         and (g["tile"] is not None or not bank_busy[g["bank"]])]
+                if not ready:
+                    break
+                g = min(ready, key=lambda g: (g["h"], RANK[g["kind"]], g["q"] if QMAJOR else 0, g["panels"][g["at"]], g["q"]))
+                if g["tile"] is None:
+                    bank_busy[g["bank"]] = True
+                    g["tile"] = bank(g["bank"], [P, N])
+                one_pass(g)
+                left -= 1
+                if g["at"] == len(g["panels"]):
+                    pending.extend([(g, 1, step)] if g["kind"] == "r0" else [(g, 1, step), (g, -1, step)])
 
-        queues = {e: sorted([n for n in range(len(program)) if program[n][0] == e], key=lambda n: (program[n][1], n))
-                  for e in ENGINES}
-        issued = set()
-        while len(issued) < len(program):
-            before = len(issued)
-            for e in ENGINES:
-                while queues[e] and behind[queues[e][0]] <= issued:
-                    n = queues[e].pop(0)
-                    program[n][4]()
-                    issued.add(n)
-            assert len(issued) > before, "the engines' orders contradict the dataflow"
+        def combine(dst, src, factor, other):
+            nc.vector.scalar_tensor_tensor(out=dst, in0=src[:], scalar=factor, in1=other, op0=MULT, op1=ADD)
+
+        def epilogue(g, sg):
+            h, q, kind = g["h"], g["q"], g["kind"]
+            if kind == "r0":
+                part["base", h, q] = sb("base%d" % q, [P, N], F32)
+                combine(part["base", h, q][:], g["tile"], 1.0 / 16, bias_sb[:, h * N : (h + 1) * N])
+                bank_busy[g["bank"]] = False
+            elif kind == "r1":
+                part["f", h, q, sg] = sb("f%d_%d" % (q, sg + 1), [P, N], F32)
+                combine(part["f", h, q, sg][:], g["tile"], sg / 16.0, part["base", h, q][:])
+                if sg < 0:
+                    bank_busy[g["bank"]] = False
+            else:
+                a = 1 if kind == "T+" else -1
+                k = z_count[0] % 16
+                z_count[0] += 1
+                if k % 4 == 0:
+                    z_tiles[k // 4] = sb("x_grp%d" % (k // 4), [P, 4, N], F32)
+                z = z_tiles[k // 4][:, k % 4, :]
+                combine(z, g["tile"], sg / 16.0, part["f", h, q, a][:])
+                p = (0 if a > 0 else 1) + (0 if sg > 0 else 2)
+                nc.sync.dma_start(out=out_view[p, q, :, :, h * N : (h + 1) * N], in_=z)
+                if sg < 0:
+                    bank_busy[g["bank"]] = False
+
+        items = list(SEQ_HEAD) + [s for s in range(PANELS) if s not in SEQ_HEAD]
+        n_items = len(items)
+        for item in items[:LOADS_AHEAD]:
+            load(item)
+
+        def is_x(item):
+            return isinstance(item, str) and item != "b"
+
+        def turn(k):
+            if 0 <= k < n_items:
+                if is_x(items[k]):
+                    x_turn(int(items[k][1]))
+                elif items[k] == "b":
+                    bias_mm()
+
+        def spread(k, n_epi):
+            if 0 <= k < n_items:
+                item = items[k]
+                if item == "b":
+                    bias_copy()
+                elif is_x(item):
+                    x_copy(int(item[1]), item == "x0")
+                else:
+                    sp = SPLIT_EARLY if item < EARLY else SPLIT[min(n_epi, 2)]
+                    interleave(item, sp[0], sp[1])
+
+        late = []
+
+        def stage2(item):
+            todo = list(late)
+            late.clear()
+            if is_x(item):
+                x_quant(int(item[1]), 0)
+                x_negate(int(item[1]))
+                late.append(int(item[1]))
+            elif item != "b":
+                if item >= CODE_BUFS:
+                    assert used[item - CODE_BUFS] == (4 if (item - CODE_BUFS) % COEFFS < 8 else 8), item
+                quantise(item)
+            for c in todo:
+                x_quant(c, 1)
+
+        for k in range(LEAD_T):
+            turn(k)
+        for k in range(LEAD):
+            spread(k, 0)
+        k = 0
+        done = -1
+        n_epi = 0
+        while k < n_items or pending or any(g["at"] < len(g["panels"]) for g in groups):
+            last = k >= n_items - 1
+            turn(k + LEAD_T)
+            if k < n_items:
+                stage2(items[k])
+                if not isinstance(items[k], str):
+                    done = items[k]
+            pe_step(done, k, last, n_epi)
+            n_epi = min(len(pending) if last else V_EPI, len(pending))
+            spread(k + LEAD, n_epi)
+            if k + LOADS_AHEAD < n_items:
+                load(items[k + LOADS_AHEAD])
+            for i in range(n_epi):
+                g, sg, at_step = pending.pop(0)
+                epilogue(g, sg)
+            k += 1

@@ -27,9 +27,14 @@ CODE_BUFS = 10
 LEAD = 2
 V_EPI = 2
 PE_BUDGET = 5
+PE_LAST = 4
+LAST_FROM = 24
 E_LAG = 0
+E_LAG_R = 0
+X_ON_V = ()
+X_ALL_V = ()
 QMAJOR = 1
-SPLIT = ((320, 0), (320, 96), (352, 160))
+SPLIT = ((320, 0), (336, 64), (352, 128))
 RANK = {"T+": 0, "T-": 1, "r0": 2, "r1": 2}
 SEQ_HEAD = ("x0", 0, "x1", 1, "x2", 2, "x3", 3, "b")
 LEAD_T = 4
@@ -103,7 +108,7 @@ def tile_iwht3layer_pa_kernel(tc, trans, weight, bias, out):
         def x_copy(c, first):
             x_grp[c] = sb("x_grp%d" % c, [P, 2, 4, C], BF16)
             for pair in range(2):
-                copy = nc.vector.tensor_copy if (first and pair == 1) else nc.scalar.copy
+                copy = nc.vector.tensor_copy if ((first or c in X_ON_V) and pair == 1) or c in X_ALL_V else nc.scalar.copy
                 copy(out=x_grp[c][:, 0, 2 * pair : 2 * pair + 2, :].bitcast(F32).rearrange("p t (r u) -> p t r u", u=2),
                      in_=turned[c, pair][:].rearrange("p t u r -> p t r u"))
 
@@ -170,7 +175,7 @@ def tile_iwht3layer_pa_kernel(tc, trans, weight, bias, out):
             used[s] += 1
 
         def pe_step(done, step, last, extra):
-            left = 1000 if last else PE_BUDGET + extra
+            left = 1000 if last else (PE_LAST if done >= LAST_FROM else PE_BUDGET) + extra
             while left > 0:
                 ready = [g for g in groups if g["at"] < len(g["panels"]) and g["panels"][g["at"]] <= done
                          and (g["tile"] is not None or not bank_busy[g["bank"]])]
@@ -269,7 +274,8 @@ def tile_iwht3layer_pa_kernel(tc, trans, weight, bias, out):
                 if not isinstance(items[k], str):
                     done = items[k]
             pe_step(done, k, last, n_epi)
-            n_epi = min(len(pending) if last else V_EPI, len(pending))
+            ripe = len([e for e in pending if e[2] + (E_LAG if e[0]["kind"][0] == "T" else E_LAG_R) <= k])
+            n_epi = len(pending) if last else min(V_EPI, ripe)
             spread(k + LEAD, n_epi)
             if k + LOADS_AHEAD < n_items:
                 load(items[k + LOADS_AHEAD])

@@ -23,18 +23,20 @@ FLOPS = 2 * COEFFS * P * C * K
 
 RAW_BUFS = 16
 GRP_BUFS = 3
-CODE_BUFS = 10
+CODE_BUFS = 12
 LEAD = 2
 V_EPI = 2
-PE_BUDGET = 5
+PE_BUDGET = 6
 PE_LAST = 4
+PE_C0 = 4
+HOLD_END = 0
 LAST_FROM = 24
 E_LAG = 0
 E_LAG_R = 0
 X_ON_V = ()
 X_ALL_V = ()
 QMAJOR = 1
-SPLIT = ((320, 0), (336, 64), (352, 128))
+SPLIT = ((320, 0), (336, 64), (352, 144))
 RANK = {"T+": 0, "T-": 1, "r0": 2, "r1": 2}
 SEQ_HEAD = ("x0", 0, "x1", 1, "x2", 2, "x3", 3, "b")
 LEAD_T = 4
@@ -175,10 +177,12 @@ def tile_iwht3layer_pa_kernel(tc, trans, weight, bias, out):
             used[s] += 1
 
         def pe_step(done, step, last, extra):
-            left = 1000 if last else (PE_LAST if done >= LAST_FROM else PE_BUDGET) + extra
+            left = 1000 if last else (PE_LAST if done >= LAST_FROM else (PE_C0 if 8 <= done < 16 else PE_BUDGET)) + extra
             while left > 0:
                 ready = [g for g in groups if g["at"] < len(g["panels"]) and g["panels"][g["at"]] <= done
                          and (g["tile"] is not None or not bank_busy[g["bank"]])]
+                if HOLD_END and not last and done >= PANELS - 1 - HOLD_END:
+                    ready = [g for g in ready if not (g["kind"] == "T+" and g["h"] == 1)]
                 if not ready:
                     break
                 g = min(ready, key=lambda g: (g["h"], RANK[g["kind"]], g["q"] if QMAJOR else 0, g["panels"][g["at"]], g["q"]))

@@ -141,6 +141,9 @@ def tile_iwht3layer_pa_kernel(tc, trans, weight, bias, out):
                 if hi == lo:
                     continue
                 dst, src = grp[s][:, lo:hi, :], raw[s][:, :, lo:hi].rearrange("p r n -> p n r")
+                if e != 1:
+                    dst = grp[s][:, lo:hi, :].rearrange("p (c i) r -> p c r i", i=4)
+                    src = raw[s][:, :, lo:hi].rearrange("p r (c i) -> p c r i", i=4)
                 if e == 0:
                     nc.scalar.copy(out=dst, in_=src)
                 elif e == 1:

@@ -10,6 +10,8 @@ U8 = mybir.dt.uint8
 MX = mybir.dt.float8_e5m2_x4
 MULT = mybir.AluOpType.mult
 ADD = mybir.AluOpType.add
+SUB = mybir.AluOpType.subtract
+COPY = mybir.ActivationFunctionType.Copy
 
 P = 128
 COEFFS = 16
@@ -25,26 +27,26 @@ RAW_BUFS = 16
 GRP_BUFS = 3
 CODE_BUFS = 12
 LEAD = 2
+LEAD_T = 6
+LEAD_G = 3
 V_EPI = 2
+LAG = 1
 PE_BUDGET = 6
 PE_LAST = 4
 PE_C0 = 4
-HOLD_END = 0
 LAST_FROM = 24
-E_LAG = 0
-E_LAG_R = 0
-X_ON_V = ()
-X_ALL_V = ()
-QMAJOR = 1
-SPLIT = ((320, 0), (336, 64), (352, 144))
-RANK = {"T+": 0, "T-": 1, "r0": 2, "r1": 2}
-SEQ_HEAD = ("x0", 0, "x1", 1, "x2", 2, "x3", 3, "b")
-LEAD_T = 4
 LOADS_AHEAD = 16
-EARLY = 8
-SPLIT_EARLY = (352, 0)
-X_BANKS = ((4, 5), (6, 7), (4, 5), (6, 7))
-BIAS_BANKS = (4, 5)
+SEQ_HEAD = (0, "x0", 1, "x1", 2, "x2", 3, "x3", "b")
+ON_TENSOR = (1, 2)
+PAIRS = ((4, 5), (6, 7), (0, 1), (2, 3))
+G_COLS = (0, 64, 144)
+S_COLS = (320, 352, 352)
+S_COLS_X = 352
+V_SMALL = 16
+G_TAIL = ()
+RANK = {"T+": 0, "T-": 1, "r0": -1, "r1": -1, "r2": 0, "r3": 0}
+PT_ON_V = 0
+X0_ON_V = 1
 
 
 def tile_iwht3layer_pa_kernel(tc, trans, weight, bias, out):
@@ -59,58 +61,78 @@ def tile_iwht3layer_pa_kernel(tc, trans, weight, bias, out):
         psum = ctx.enter_context(tc.psum_pool(name="psum", bufs=1))
 
         ident = sbuf.tile([P, P], F32, name="ident")
+        ident_bf = sbuf.tile([P, P], BF16, name="ident_bf")
         ones = sbuf.tile([P, P], BF16, name="ones")
         bias_pad = sbuf.tile([P, K], BF16, name="bias_pad")
-        bias_sb = sbuf.tile([P, K], F32, name="bias_sb")
+        bias_sb = sbuf.tile([P, K], BF16, name="bias_sb")
         x_codes = sbuf.tile([P, 4, 1024], U32, name="x_codes", align_bytes=64)
         x_scales = sbuf.tile([P, 4, 1024], U8, name="x_scales", align_bytes=64)
         make_identity(nc, ident[:])
+        if ON_TENSOR:
+            make_identity(nc, ident_bf[:])
         nc.gpsimd.memset(bias_pad[:], 0.0)
         nc.gpsimd.memset(ones[:], 1.0)
         ctx.enter_context(tc.manual_schedule())
 
         raw, grp, wc, ws, x_raw, x_grp = {}, {}, {}, {}, {}, {}
         bank_busy = [False] * 8
+        written = set()
 
         def sb(tag, shape, dtype):
             return sbuf.tile(shape, dtype, name=tag, align_bytes=64)
 
-        def bank(b, shape):
-            return psum.tile(shape, F32, name="bank%d" % b)
-
-        def load_x(c):
-            x_raw[c] = sb("x_raw%d" % c, [P, 4, C], BF16)
-            nc.sync.dma_start(out=x_raw[c][:], in_=x_view[:, 4 * c : 4 * c + 4, :])
+        def bank(b, shape, dtype=F32):
+            assert not bank_busy[b], b
+            return psum.tile(shape, dtype, name="bank%d" % b)
 
         def load(item):
             if item == "b":
                 nc.sync.dma_start(out=bias_pad[0:1, :], in_=bias_row)
             elif isinstance(item, str):
-                load_x(int(item[1]))
+                c = int(item[1])
+                x_raw[c] = sb("x_raw%d" % c, [P, 4, C], BF16)
+                nc.sync.dma_start(out=x_raw[c][:], in_=x_view[:, 4 * c : 4 * c + 4, :])
             else:
-                load_w(item)
-
-        def load_w(s):
-            h, t = divmod(s, COEFFS)
-            raw[s] = sb("raw%d" % (s % RAW_BUFS), [P, 4, N], BF16)
-            nc.sync.dma_start(out=raw[s][:], in_=w_view[t, :, :, h * N : (h + 1) * N])
+                h, t = divmod(item, COEFFS)
+                raw[item] = sb("raw%d" % (item % RAW_BUFS), [P, 4, N], BF16)
+                nc.sync.dma_start(out=raw[item][:], in_=w_view[t, :, :, h * N : (h + 1) * N])
 
         turned = {}
+        pair_at = [0]
+
+        held = {}
+
+        def next_pair(item):
+            banks = PAIRS[pair_at[0] % len(PAIRS)]
+            pair_at[0] += 1
+            held[item] = banks
+            return banks
+
+        def pair_free():
+            return not any(bank_busy[b] for b in PAIRS[pair_at[0] % len(PAIRS)])
+
+        def hold(item):
+            for b in held[item]:
+                bank_busy[b] = True
+
+        def release(item):
+            for b in held[item]:
+                bank_busy[b] = False
 
         def x_turn(c):
             words = x_raw[c][:].bitcast(F32)
+            banks = next_pair("x%d" % c)
             for pair in range(2):
-                assert not bank_busy[X_BANKS[c][pair]]
-                xt = bank(X_BANKS[c][pair], [P, 2, 2, P])
+                xt = bank(banks[pair], [P, 2, 2, P])
                 turned[c, pair] = xt
                 for tt in range(2):
                     for u in range(2):
                         nc.tensor.transpose(xt[:, tt, u, :], words[:, 2 * pair + tt, u : C // 2 : 2], ident[:])
 
-        def x_copy(c, first):
+        def x_copy(c):
             x_grp[c] = sb("x_grp%d" % c, [P, 2, 4, C], BF16)
             for pair in range(2):
-                copy = nc.vector.tensor_copy if ((first or c in X_ON_V) and pair == 1) or c in X_ALL_V else nc.scalar.copy
+                copy = nc.vector.tensor_copy if (X0_ON_V and c == 0 and pair == 1) else nc.scalar.copy
                 copy(out=x_grp[c][:, 0, 2 * pair : 2 * pair + 2, :].bitcast(F32).rearrange("p t (r u) -> p t r u", u=2),
                      in_=turned[c, pair][:].rearrange("p t u r -> p t r u"))
 
@@ -124,32 +146,42 @@ def tile_iwht3layer_pa_kernel(tc, trans, weight, bias, out):
                                         in0=x_grp[c][:, 0, :, :].rearrange("p t k -> p (t k)"), scalar1=-1.0)
 
         def bias_mm():
+            turned["b"] = bank(next_pair("b")[0], [P, K], BF16)
             for h in range(HALVES):
-                assert not bank_busy[BIAS_BANKS[h]]
-                turned["b", h] = bank(BIAS_BANKS[h], [P, N])
-                nc.tensor.matmul(out=turned["b", h][:], lhsT=ones[:], rhs=bias_pad[:, h * N : (h + 1) * N], start=True, stop=True)
+                nc.tensor.matmul(out=turned["b"][:, h * N : (h + 1) * N], lhsT=ones[:], rhs=bias_pad[:, h * N : (h + 1) * N], start=True, stop=True)
 
         def bias_copy():
-            for h in range(HALVES):
-                nc.scalar.copy(out=bias_sb[:, h * N : (h + 1) * N], in_=turned["b", h][:])
+            nc.scalar.copy(out=bias_sb[:], in_=turned["b"][:])
+            written.add("b")
 
-        def interleave(s, s_cols, g_cols):
-            grp[s] = sb("grp%d" % (s % GRP_BUFS), [P, N, 4], BF16)
-            cuts = (0, s_cols, s_cols + g_cols, N)
-            for e in range(3):
-                lo, hi = cuts[e], cuts[e + 1]
-                if hi == lo:
-                    continue
-                dst, src = grp[s][:, lo:hi, :], raw[s][:, :, lo:hi].rearrange("p r n -> p n r")
-                if e != 1:
-                    dst = grp[s][:, lo:hi, :].rearrange("p (c i) r -> p c r i", i=4)
-                    src = raw[s][:, :, lo:hi].rearrange("p r (c i) -> p c r i", i=4)
-                if e == 0:
-                    nc.scalar.copy(out=dst, in_=src)
-                elif e == 1:
-                    nc.gpsimd.tensor_scalar(out=dst, in0=src, scalar1=1.0, scalar2=0.0, op0=MULT, op1=ADD)
-                else:
-                    nc.vector.tensor_copy(out=dst, in_=src)
+        def w_turn(s):
+            banks = next_pair(s)
+            for i in range(2):
+                laid = bank(banks[i], [P, 2 * N], BF16)
+                turned["w", s, i] = laid
+                for j in range(2):
+                    lo = 256 * i + 128 * j
+                    nc.tensor.matmul(out=laid[:, N * j : N * (j + 1)], lhsT=ident_bf[:], rhs=raw[s][:, :, lo : lo + 128].rearrange("p r n -> p n r"),
+                                     start=True, stop=True)
+
+        def slot(s):
+            if s not in grp:
+                grp[s] = sb("grp%d" % (s % GRP_BUFS), [P, N, 4], BF16)
+            return grp[s]
+
+        def part_copy(s, engine, lo, hi):
+            if hi == lo:
+                return
+            dst, src = slot(s)[:, lo:hi, :], raw[s][:, :, lo:hi].rearrange("p r n -> p n r")
+            if engine != "g":
+                dst = slot(s)[:, lo:hi, :].rearrange("p (c i) r -> p c r i", i=4)
+                src = raw[s][:, :, lo:hi].rearrange("p r (c i) -> p c r i", i=4)
+            if engine == "s":
+                nc.scalar.copy(out=dst, in_=src)
+            elif engine == "g":
+                nc.gpsimd.tensor_scalar(out=dst, in0=src, scalar1=1.0, scalar2=0.0, op0=MULT, op1=ADD)
+            else:
+                nc.vector.tensor_copy(out=dst, in_=src)
 
         def quantise(s):
             wc[s] = sb("w_codes%d" % (s % CODE_BUFS), [P, N], U32)
@@ -160,9 +192,12 @@ def tile_iwht3layer_pa_kernel(tc, trans, weight, bias, out):
         for h in range(HALVES):
             for kind, first, count, b0 in (("r0", 0, 4, 0), ("r1", 4, 4, 4), ("T+", 8, 8, 0), ("T-", 8, 8, 4)):
                 for q in range(4):
+                    if h == 1 and q in G_TAIL and kind[0] == "T":
+                        kind2, first2 = ("r2", 8) if kind == "T+" else ("r3", 12)
+                        groups.append({"kind": kind2, "h": h, "q": q, "bank": b0 + q, "panels": [COEFFS * h + first2 + i for i in range(4)], "at": 0, "tile": None})
+                        continue
                     groups.append({"kind": kind, "h": h, "q": q, "bank": b0 + q, "panels": [COEFFS * h + first + i for i in range(count)],
                                    "at": 0, "tile": None})
-        used = [0] * PANELS
         pending = []
         part = {}
         z_count = [0]
@@ -177,28 +212,32 @@ def tile_iwht3layer_pa_kernel(tc, trans, weight, bias, out):
             nc.tensor.matmul_mx(out=g["tile"][:], lhsT=x_codes[:, t // 4, lo : lo + P].bitcast(MX), lhsT_scale=x_scales[:, t // 4, lo : lo + P],
                                 rhs=wc[s][:].bitcast(MX), rhs_scale=ws[s][:], start=g["at"] == 0, stop=g["at"] == len(g["panels"]) - 1)
             g["at"] += 1
-            used[s] += 1
 
-        def pe_step(done, step, last, extra):
+        def pe_step(done, last, extra, step):
             left = 1000 if last else (PE_LAST if done >= LAST_FROM else (PE_C0 if 8 <= done < 16 else PE_BUDGET)) + extra
             while left > 0:
                 ready = [g for g in groups if g["at"] < len(g["panels"]) and g["panels"][g["at"]] <= done
-                         and (g["tile"] is not None or not bank_busy[g["bank"]])]
-                if HOLD_END and not last and done >= PANELS - 1 - HOLD_END:
-                    ready = [g for g in ready if not (g["kind"] == "T+" and g["h"] == 1)]
+                         and (g["panels"][g["at"]] % COEFFS) // 4 in written and (g["tile"] is not None or not bank_busy[g["bank"]])]
                 if not ready:
                     break
-                g = min(ready, key=lambda g: (g["h"], RANK[g["kind"]], g["q"] if QMAJOR else 0, g["panels"][g["at"]], g["q"]))
+                g = min(ready, key=lambda g: (g["h"], RANK[g["kind"]], g["q"], g["panels"][g["at"]]))
                 if g["tile"] is None:
-                    bank_busy[g["bank"]] = True
                     g["tile"] = bank(g["bank"], [P, N])
+                    bank_busy[g["bank"]] = True
                 one_pass(g)
                 left -= 1
                 if g["at"] == len(g["panels"]):
-                    pending.extend([(g, 1, step)] if g["kind"] == "r0" else [(g, 1, step), (g, -1, step)])
+                    pending.extend([(g, 1, step)] if g["kind"] in ("r0", "r2", "r3") else [(g, 1, step), (g, -1, step)])
 
         def combine(dst, src, factor, other):
             nc.vector.scalar_tensor_tensor(out=dst, in0=src[:], scalar=factor, in1=other, op0=MULT, op1=ADD)
+
+        def result_tile():
+            k = z_count[0] % 16
+            z_count[0] += 1
+            if k % 4 == 0:
+                z_tiles[k // 4] = sb("x_grp%d" % (k // 4), [P, 4, N], F32)
+            return z_tiles[k // 4][:, k % 4, :]
 
         def epilogue(g, sg):
             h, q, kind = g["h"], g["q"], g["kind"]
@@ -211,44 +250,88 @@ def tile_iwht3layer_pa_kernel(tc, trans, weight, bias, out):
                 combine(part["f", h, q, sg][:], g["tile"], sg / 16.0, part["base", h, q][:])
                 if sg < 0:
                     bank_busy[g["bank"]] = False
+            elif kind in ("r2", "r3"):
+                part[kind, h, q] = sb("%s_%d" % (kind, q), [P, N], F32)
+                nc.scalar.activation(out=part[kind, h, q][:], in_=g["tile"][:], func=COPY, scale=1.0 / 16)
+                bank_busy[g["bank"]] = False
+                if kind == "r3":
+                    for a in (1, -1):
+                        b = sb("b%d_%d" % (q, a + 1), [P, N], F32)
+                        nc.gpsimd.tensor_tensor(out=b[:], in0=part["r2", h, q][:], in1=part["r3", h, q][:], op=ADD if a > 0 else SUB)
+                        for s2 in (1, -1):
+                            z = result_tile()
+                            nc.gpsimd.tensor_tensor(out=z, in0=part["f", h, q, a][:], in1=b[:], op=ADD if s2 > 0 else SUB)
+                            nc.scalar.dma_start(out=out_view[(0 if a > 0 else 1) + (0 if s2 > 0 else 2), q, :, :, h * N : (h + 1) * N], in_=z)
             else:
                 a = 1 if kind == "T+" else -1
-                k = z_count[0] % 16
-                z_count[0] += 1
-                if k % 4 == 0:
-                    z_tiles[k // 4] = sb("x_grp%d" % (k // 4), [P, 4, N], F32)
-                z = z_tiles[k // 4][:, k % 4, :]
+                z = result_tile()
                 combine(z, g["tile"], sg / 16.0, part["f", h, q, a][:])
-                p = (0 if a > 0 else 1) + (0 if sg > 0 else 2)
-                nc.sync.dma_start(out=out_view[p, q, :, :, h * N : (h + 1) * N], in_=z)
+                nc.sync.dma_start(out=out_view[(0 if a > 0 else 1) + (0 if sg > 0 else 2), q, :, :, h * N : (h + 1) * N], in_=z)
                 if sg < 0:
                     bank_busy[g["bank"]] = False
 
+        def on_vector(e):
+            return e[0]["kind"] not in ("r2", "r3")
+
         items = list(SEQ_HEAD) + [s for s in range(PANELS) if s not in SEQ_HEAD]
         n_items = len(items)
+        panel_step = {}
+        for k in range(n_items):
+            panel_step[items[k]] = k
         for item in items[:LOADS_AHEAD]:
             load(item)
 
         def is_x(item):
             return isinstance(item, str) and item != "b"
 
-        def turn(k):
-            if 0 <= k < n_items:
-                if is_x(items[k]):
-                    x_turn(int(items[k][1]))
-                elif items[k] == "b":
-                    bias_mm()
+        turn_at = [0]
 
-        def spread(k, n_epi):
+        def turns(upto):
+            while turn_at[0] < min(upto, n_items):
+                item = items[turn_at[0]]
+                if isinstance(item, str) or item in ON_TENSOR:
+                    if not pair_free():
+                        break
+                    if is_x(item):
+                        x_turn(int(item[1]))
+                    elif item == "b":
+                        bias_mm()
+                    else:
+                        w_turn(item)
+                    hold(item)
+                turn_at[0] += 1
+
+        g_cols = {}
+        v_cols = {}
+
+        def spread_s(k):
             if 0 <= k < n_items:
                 item = items[k]
+                assert turn_at[0] > k
                 if item == "b":
                     bias_copy()
+                    release(item)
                 elif is_x(item):
-                    x_copy(int(item[1]), item == "x0")
+                    x_copy(int(item[1]))
+                    release(item)
+                elif item in ON_TENSOR:
+                    for i in range(2):
+                        copy = nc.vector.tensor_copy if (PT_ON_V and i == 1) else nc.scalar.copy
+                        copy(out=slot(item)[:, 256 * i : 256 * (i + 1), :].rearrange("p n r -> p (n r)"), in_=turned["w", item, i][:])
+                    release(item)
                 else:
-                    sp = SPLIT_EARLY if item < EARLY else SPLIT[min(n_epi, 2)]
-                    interleave(item, sp[0], sp[1])
+                    part_copy(item, "s", g_cols.get(item, 0), N - v_cols[item])
+
+        def spread_v(k, n_epi, x_work, when):
+            if 0 <= k < n_items and not isinstance(items[k], str) and items[k] not in ON_TENSOR:
+                v_cols[items[k]] = N - g_cols.get(items[k], 0) - (S_COLS_X if x_work else S_COLS[min(n_epi, 2)])
+                if when == (v_cols[items[k]] <= V_SMALL or n_epi == 0):
+                    part_copy(items[k], "v", N - v_cols[items[k]], N)
+
+        def spread_g(s, n_epi):
+            if s < PANELS and s not in ON_TENSOR and G_COLS[min(n_epi, 2)]:
+                g_cols[s] = G_COLS[min(n_epi, 2)]
+                part_copy(s, "g", 0, g_cols[s])
 
         late = []
 
@@ -260,33 +343,43 @@ def tile_iwht3layer_pa_kernel(tc, trans, weight, bias, out):
                 x_negate(int(item[1]))
                 late.append(int(item[1]))
             elif item != "b":
-                if item >= CODE_BUFS:
-                    assert used[item - CODE_BUFS] == (4 if (item - CODE_BUFS) % COEFFS < 8 else 8), item
                 quantise(item)
             for c in todo:
                 x_quant(c, 1)
+                written.add(c)
 
-        for k in range(LEAD_T):
-            turn(k)
         for k in range(LEAD):
-            spread(k, 0)
+            turns(k + LEAD_T)
+            spread_v(k, 0, True, True)
+            spread_s(k)
         k = 0
         done = -1
         n_epi = 0
         while k < n_items or pending or any(g["at"] < len(g["panels"]) for g in groups):
             last = k >= n_items - 1
-            turn(k + LEAD_T)
-            if k < n_items:
-                stage2(items[k])
-                if not isinstance(items[k], str):
-                    done = items[k]
-            pe_step(done, k, last, n_epi)
-            ripe = len([e for e in pending if e[2] + (E_LAG if e[0]["kind"][0] == "T" else E_LAG_R) <= k])
-            n_epi = len(pending) if last else min(V_EPI, ripe)
-            spread(k + LEAD, n_epi)
+            item = items[k] if k < n_items else None
+            turns(k + LEAD + LEAD_T)
+            x_work = bool(late) or (item is not None and is_x(item))
+            if item is not None:
+                stage2(item)
+                if not isinstance(item, str):
+                    done = item
+            pe_step(done, last, n_epi, k)
+            ripe = 0
+            for e in pending:
+                if (e[0]["kind"] == "r0" and "b" not in written) or (e[2] + LAG > k and not last):
+                    break
+                ripe += 1
+            n_epi = ripe if last else min(V_EPI, ripe)
+            n_v = len([e for e in pending[:n_epi] if on_vector(e)])
+            if item is not None and not isinstance(item, str):
+                spread_g(item + LEAD_G, n_v)
+            spread_v(k + LEAD, n_v, x_work, True)
+            spread_s(k + LEAD)
             if k + LOADS_AHEAD < n_items:
                 load(items[k + LOADS_AHEAD])
             for i in range(n_epi):
                 g, sg, at_step = pending.pop(0)
                 epilogue(g, sg)
+            spread_v(k + LEAD, n_v, x_work, False)
             k += 1

@@ -37,7 +37,7 @@ PE_C0 = 4
 LAST_FROM = 24
 LOADS_AHEAD = 16
 SEQ_HEAD = (0, "x0", 1, "x1", 2, "x2", 3, "x3", "b")
-ON_TENSOR = (1, 2)
+ON_TENSOR = ()
 PAIRS = ((4, 5), (6, 7), (0, 1), (2, 3))
 G_COLS = (0, 64, 144)
 S_COLS = (320, 352, 352)

@@ -30,21 +30,26 @@ LEAD = 2
 LEAD_T = 6
 LEAD_G = 3
 V_EPI = 2
+V_BURST = 3
+BURST = ("SA", "P+")
 LAG = 1
 PE_BUDGET = 6
-PE_LAST = 4
+PE_LAST = 3
 PE_C0 = 4
 LAST_FROM = 24
 LOADS_AHEAD = 16
-SEQ_HEAD = (0, "x0", 1, "x1", 2, "x2", 3, "x3", "b")
+SEQ_HEAD = ("x0", 0, "x1", 1, "x2", 2, "x3", 3, "b")
 ON_TENSOR = ()
-PAIRS = ((4, 5), (6, 7), (0, 1), (2, 3))
+PAIRS = ((4, 5), (6, 7))
 G_COLS = (0, 64, 144)
-S_COLS = (320, 352, 352)
+S_COLS = (256, 320, 352)
 S_COLS_X = 352
 V_SMALL = 16
 G_TAIL = ()
-RANK = {"T+": 0, "T-": 1, "r0": -1, "r1": -1, "r2": 0, "r3": 0}
+RANK = {"T+": 0, "T-": 1, "SA": -3, "P+": -2, "P-": -1, "r2": 0, "r3": 0}
+SPLIT_T = ((0, 3), (1, 3))
+ON_G = ((1, 3),)
+NEG = (2, 3)
 PT_ON_V = 0
 X0_ON_V = 1
 
@@ -190,15 +195,22 @@ def tile_iwht3layer_pa_kernel(tc, trans, weight, bias, out):
 
         groups = []
         for h in range(HALVES):
-            for kind, first, count, b0 in (("r0", 0, 4, 0), ("r1", 4, 4, 4), ("T+", 8, 8, 0), ("T-", 8, 8, 4)):
+            for q in range(4):
+                plus = [4 * u + v for u in range(2) for v in range(4) if HAD[q][v] > 0]
+                minus = [4 * u + v for u in range(2) for v in range(4) if HAD[q][v] * (1 - 2 * u) > 0]
+                groups.append({"kind": "SA" if q == 0 else "P+", "h": h, "q": q, "bank": q, "panels": [COEFFS * h + t for t in plus], "at": 0, "tile": None})
+                groups.append({"kind": "P-", "h": h, "q": q, "bank": 4 + q, "panels": [COEFFS * h + t for t in minus], "at": 0, "tile": None})
+            for kind, b0 in (("T+", 0), ("T-", 4)):
                 for q in range(4):
-                    if h == 1 and q in G_TAIL and kind[0] == "T":
-                        kind2, first2 = ("r2", 8) if kind == "T+" else ("r3", 12)
-                        groups.append({"kind": kind2, "h": h, "q": q, "bank": b0 + q, "panels": [COEFFS * h + first2 + i for i in range(4)], "at": 0, "tile": None})
+                    if (h, q) in SPLIT_T:
+                        first = 8 if kind == "T+" else 12
+                        groups.append({"kind": "r2" if kind == "T+" else "r3", "h": h, "q": q, "bank": b0 + q, "panels": [COEFFS * h + first + i for i in range(4)], "at": 0, "tile": None})
                         continue
-                    groups.append({"kind": kind, "h": h, "q": q, "bank": b0 + q, "panels": [COEFFS * h + first + i for i in range(count)],
-                                   "at": 0, "tile": None})
+                    groups.append({"kind": kind, "h": h, "q": q, "bank": b0 + q, "panels": [COEFFS * h + 8 + i for i in range(8)], "at": 0, "tile": None})
+        turn_at = [0]
         pending = []
+        waiting = []
+        closed = set()
         part = {}
         z_count = [0]
         z_tiles = {}
@@ -207,7 +219,7 @@ def tile_iwht3layer_pa_kernel(tc, trans, weight, bias, out):
             s = g["panels"][g["at"]]
             t = s % COEFFS
             u, v = divmod(t, 4)
-            sign = HAD[g["q"]][v] * (-1 if (g["kind"] == "T-" and u == 3) else 1)
+            sign = HAD[g["q"]][v] * (-1 if (g["kind"] == "T-" and u == 3) else 1) if g["kind"][0] in "Tr" else 1
             lo = (0 if sign > 0 else 512) + (t % 4) * P
             nc.tensor.matmul_mx(out=g["tile"][:], lhsT=x_codes[:, t // 4, lo : lo + P].bitcast(MX), lhsT_scale=x_scales[:, t // 4, lo : lo + P],
                                 rhs=wc[s][:].bitcast(MX), rhs_scale=ws[s][:], start=g["at"] == 0, stop=g["at"] == len(g["panels"]) - 1)
@@ -217,7 +229,7 @@ def tile_iwht3layer_pa_kernel(tc, trans, weight, bias, out):
             left = 1000 if last else (PE_LAST if done >= LAST_FROM else (PE_C0 if 8 <= done < 16 else PE_BUDGET)) + extra
             while left > 0:
                 ready = [g for g in groups if g["at"] < len(g["panels"]) and g["panels"][g["at"]] <= done
-                         and (g["panels"][g["at"]] % COEFFS) // 4 in written and (g["tile"] is not None or not bank_busy[g["bank"]])]
+                         and (g["panels"][g["at"]] % COEFFS) // 4 in written and (g["tile"] is not None or (not bank_busy[g["bank"]] and (g["bank"] < 4 or turn_at[0] >= len(SEQ_HEAD))))]
                 if not ready:
                     break
                 g = min(ready, key=lambda g: (g["h"], RANK[g["kind"]], g["q"], g["panels"][g["at"]]))
@@ -227,7 +239,16 @@ def tile_iwht3layer_pa_kernel(tc, trans, weight, bias, out):
                 one_pass(g)
                 left -= 1
                 if g["at"] == len(g["panels"]):
-                    pending.extend([(g, 1, step)] if g["kind"] in ("r0", "r2", "r3") else [(g, 1, step), (g, -1, step)])
+                    if g["kind"][0] == "P":
+                        (pending if ("SA", g["h"]) in closed else waiting).append((g, 1, step))
+                    elif g["kind"][0] == "r":
+                        pending.extend([(g, 0, step)] if (g["h"], g["q"]) in ON_G else [(g, i, step) for i in range(4)])
+                    else:
+                        pending.extend([(g, -1, step), (g, 1, step)] if g["kind"] == "SA" else [(g, 1, step), (g, -1, step)])
+                        if g["kind"] == "SA":
+                            closed.add(("SA", g["h"]))
+                            pending.extend([(e[0], e[1], step) for e in sorted(waiting, key=lambda e: (RANK[e[0]["kind"]], e[0]["q"]))])
+                            waiting.clear()
 
         def combine(dst, src, factor, other):
             nc.vector.scalar_tensor_tensor(out=dst, in0=src[:], scalar=factor, in1=other, op0=MULT, op1=ADD)
@@ -241,14 +262,27 @@ def tile_iwht3layer_pa_kernel(tc, trans, weight, bias, out):
 
         def epilogue(g, sg):
             h, q, kind = g["h"], g["q"], g["kind"]
-            if kind == "r0":
-                part["base", h, q] = sb("base%d" % q, [P, N], F32)
-                combine(part["base", h, q][:], g["tile"], 1.0 / 16, bias_sb[:, h * N : (h + 1) * N])
+            if kind == "SA":
+                key = ("c", h) if sg < 0 else ("f", h, 0, 1)
+                part[key] = sb("c_all" if sg < 0 else "f0_2", [P, N], F32)
+                combine(part[key][:], g["tile"], sg / 16.0, bias_sb[:, h * N : (h + 1) * N])
+                if sg > 0:
+                    bank_busy[g["bank"]] = False
+            elif kind[0] == "P":
+                a = 1 if kind == "P+" else -1
+                part["f", h, q, a] = sb("f%d_%d" % (q, a + 1), [P, N], F32)
+                combine(part["f", h, q, a][:], g["tile"], 1.0 / 8, part["c", h][:])
                 bank_busy[g["bank"]] = False
-            elif kind == "r1":
-                part["f", h, q, sg] = sb("f%d_%d" % (q, sg + 1), [P, N], F32)
-                combine(part["f", h, q, sg][:], g["tile"], sg / 16.0, part["base", h, q][:])
-                if sg < 0:
+            elif kind in ("r2", "r3") and (h, q) not in ON_G:
+                a = 1 if sg % 2 == 0 else -1
+                if kind == "r2":
+                    part["e", h, q, sg] = sb("e%d_%d" % (q, sg), [P, N], F32)
+                    combine(part["e", h, q, sg][:], g["tile"], HAD[sg][2] / 16.0, part["f", h, q, a][:])
+                else:
+                    z = result_tile()
+                    combine(z, g["tile"], HAD[sg][3] / 16.0, part["e", h, q, sg][:])
+                    nc.sync.dma_start(out=out_view[sg, q, :, :, h * N : (h + 1) * N], in_=z)
+                if sg == 3:
                     bank_busy[g["bank"]] = False
             elif kind in ("r2", "r3"):
                 part[kind, h, q] = sb("%s_%d" % (kind, q), [P, N], F32)
@@ -271,7 +305,7 @@ def tile_iwht3layer_pa_kernel(tc, trans, weight, bias, out):
                     bank_busy[g["bank"]] = False
 
         def on_vector(e):
-            return e[0]["kind"] not in ("r2", "r3")
+            return e[0]["kind"] not in ("r2", "r3") or (e[0]["h"], e[0]["q"]) not in ON_G
 
         items = list(SEQ_HEAD) + [s for s in range(PANELS) if s not in SEQ_HEAD]
         n_items = len(items)
@@ -283,8 +317,6 @@ def tile_iwht3layer_pa_kernel(tc, trans, weight, bias, out):
 
         def is_x(item):
             return isinstance(item, str) and item != "b"
-
-        turn_at = [0]
 
         def turns(upto):
             while turn_at[0] < min(upto, n_items):
@@ -340,8 +372,11 @@ def tile_iwht3layer_pa_kernel(tc, trans, weight, bias, out):
             late.clear()
             if is_x(item):
                 x_quant(int(item[1]), 0)
-                x_negate(int(item[1]))
-                late.append(int(item[1]))
+                if int(item[1]) in NEG:
+                    x_negate(int(item[1]))
+                    late.append(int(item[1]))
+                else:
+                    written.add(int(item[1]))
             elif item != "b":
                 quantise(item)
             for c in todo:
@@ -367,10 +402,11 @@ def tile_iwht3layer_pa_kernel(tc, trans, weight, bias, out):
             pe_step(done, last, n_epi, k)
             ripe = 0
             for e in pending:
-                if (e[0]["kind"] == "r0" and "b" not in written) or (e[2] + LAG > k and not last):
+                if "b" not in written or (e[2] + LAG > k and not last):
                     break
                 ripe += 1
-            n_epi = ripe if last else min(V_EPI, ripe)
+            burst = len([e for e in pending[:ripe] if e[0]["kind"] in BURST])
+            n_epi = ripe if last else max(min(V_EPI, ripe), min(burst, V_BURST))
             n_v = len([e for e in pending[:n_epi] if on_vector(e)])
             if item is not None and not isinstance(item, str):
                 spread_g(item + LEAD_G, n_v)

@@ -32,9 +32,9 @@ LEAD_G = 3
 V_EPI = 2
 V_BURST = 3
 BURST = ("SA", "P+")
-LAG = 1
+LAG = 2
 PE_BUDGET = 6
-PE_LAST = 3
+PE_LAST = 4
 PE_C0 = 4
 LAST_FROM = 24
 LOADS_AHEAD = 16

@@ -32,6 +32,7 @@ LEAD_G = 3
 V_EPI = 2
 V_BURST = 3
 BURST = ("SA", "P+")
+SPLIT_Q = 2
 LAG = 2
 PE_BUDGET = 6
 PE_LAST = 4
@@ -41,10 +42,10 @@ LOADS_AHEAD = 16
 SEQ_HEAD = ("x0", 0, "x1", 1, "x2", 2, "x3", 3, "b")
 ON_TENSOR = ()
 PAIRS = ((4, 5), (6, 7))
-G_COLS = (0, 64, 144)
+G_COLS = (0, 64, 160)
 S_COLS = (256, 320, 352)
 S_COLS_X = 352
-V_SMALL = 16
+V_SMALL = 0
 G_TAIL = ()
 RANK = {"T+": 0, "T-": 1, "SA": -3, "P+": -2, "P-": -1, "r2": 0, "r3": 0}
 SPLIT_T = ((0, 3), (1, 3))
@@ -80,6 +81,7 @@ def tile_iwht3layer_pa_kernel(tc, trans, weight, bias, out):
         ctx.enter_context(tc.manual_schedule())
 
         raw, grp, wc, ws, x_raw, x_grp = {}, {}, {}, {}, {}, {}
+        grp_all = sbuf.tile([P, GRP_BUFS, N, 4], BF16, name="grp_all", align_bytes=64)
         bank_busy = [False] * 8
         written = set()
 
@@ -170,9 +172,7 @@ def tile_iwht3layer_pa_kernel(tc, trans, weight, bias, out):
                                      start=True, stop=True)
 
         def slot(s):
-            if s not in grp:
-                grp[s] = sb("grp%d" % (s % GRP_BUFS), [P, N, 4], BF16)
-            return grp[s]
+            return grp_all[:, s % GRP_BUFS, :, :]
 
         def part_copy(s, engine, lo, hi):
             if hi == lo:
@@ -188,10 +188,13 @@ def tile_iwht3layer_pa_kernel(tc, trans, weight, bias, out):
             else:
                 nc.vector.tensor_copy(out=dst, in_=src)
 
-        def quantise(s):
+        def quantise(s, pieces):
             wc[s] = sb("w_codes%d" % (s % CODE_BUFS), [P, N], U32)
             ws[s] = sb("w_scales%d" % (s % CODE_BUFS), [P, N], U8)
-            nc.vector.quantize_mx(out=wc[s][:].bitcast(MX), scales=ws[s][:], in_=grp[s][:].rearrange("p n r -> p (n r)"))
+            w = N // pieces
+            for i in range(pieces):
+                nc.vector.quantize_mx(out=wc[s][:, i * w : (i + 1) * w].bitcast(MX), scales=ws[s][:, i * w : (i + 1) * w],
+                                      in_=slot(s)[:, i * w : (i + 1) * w, :].rearrange("p n r -> p (n r)"))
 
         groups = []
         for h in range(HALVES):
@@ -357,7 +360,7 @@ def tile_iwht3layer_pa_kernel(tc, trans, weight, bias, out):
         def spread_v(k, n_epi, x_work, when):
             if 0 <= k < n_items and not isinstance(items[k], str) and items[k] not in ON_TENSOR:
                 v_cols[items[k]] = N - g_cols.get(items[k], 0) - (S_COLS_X if x_work else S_COLS[min(n_epi, 2)])
-                if when == (v_cols[items[k]] <= V_SMALL or n_epi == 0):
+                if when == (v_cols[items[k]] <= V_SMALL or n_epi == 0) and v_cols[items[k]] > 0:
                     part_copy(items[k], "v", N - v_cols[items[k]], N)
 
         def spread_g(s, n_epi):
@@ -367,7 +370,7 @@ def tile_iwht3layer_pa_kernel(tc, trans, weight, bias, out):
 
         late = []
 
-        def stage2(item):
+        def stage2(item, pieces):
             todo = list(late)
             late.clear()
             if is_x(item):
@@ -378,7 +381,7 @@ def tile_iwht3layer_pa_kernel(tc, trans, weight, bias, out):
                 else:
                     written.add(int(item[1]))
             elif item != "b":
-                quantise(item)
+                quantise(item, pieces)
             for c in todo:
                 x_quant(c, 1)
                 written.add(c)
@@ -395,8 +398,9 @@ def tile_iwht3layer_pa_kernel(tc, trans, weight, bias, out):
             item = items[k] if k < n_items else None
             turns(k + LEAD + LEAD_T)
             x_work = bool(late) or (item is not None and is_x(item))
+            ahead = len([e for e in pending if e[2] + LAG <= k and on_vector(e)])
             if item is not None:
-                stage2(item)
+                stage2(item, SPLIT_Q if (ahead and not last and "b" in written) else 1)
                 if not isinstance(item, str):
                     done = item
             pe_step(done, last, n_epi, k)

@@ -42,8 +42,8 @@ LOADS_AHEAD = 16
 SEQ_HEAD = ("x0", 0, "x1", 1, "x2", 2, "x3", 3, "b")
 ON_TENSOR = ()
 PAIRS = ((4, 5), (6, 7))
-G_COLS = (0, 64, 160)
-S_COLS = (256, 320, 352)
+G_COLS = (0, 64, 176)
+S_COLS = (256, 320, 336)
 S_COLS_X = 352
 V_SMALL = 0
 G_TAIL = ()

from contextlib import ExitStack

import concourse.mybir as mybir
from concourse.masks import make_identity

F32 = mybir.dt.float32
BF16 = mybir.dt.bfloat16
U32 = mybir.dt.uint32
U8 = mybir.dt.uint8
MX = mybir.dt.float8_e5m2_x4
MULT = mybir.AluOpType.mult
ADD = mybir.AluOpType.add
SUB = mybir.AluOpType.subtract
COPY = mybir.ActivationFunctionType.Copy

P = 128
COEFFS = 16
C = 512
K = 1024
N = 512
HALVES = K // N
PANELS = COEFFS * HALVES
HAD = ((1, 1, 1, 1), (1, -1, 1, -1), (1, 1, -1, -1), (1, -1, -1, 1))
FLOPS = 2 * COEFFS * P * C * K

RAW_BUFS = 16
GRP_BUFS = 3
CODE_BUFS = 12
LEAD = 2
LEAD_T = 6
LEAD_G = 3
V_EPI = 2
V_BURST = 3
BURST = ("SA", "P+")
SPLIT_Q = 2
LAG = 2
PE_BUDGET = 6
PE_LAST = 4
PE_C0 = 4
LAST_FROM = 24
LOADS_AHEAD = 16
SEQ_HEAD = ("x0", 0, "x1", 1, "x2", 2, "x3", 3, "b")
ON_TENSOR = ()
PAIRS = ((4, 5), (6, 7))
G_COLS = (0, 64, 176)
S_COLS = (256, 320, 336)
S_COLS_X = 352
V_SMALL = 0
G_TAIL = ()
RANK = {"T+": 0, "T-": 1, "SA": -3, "P+": -2, "P-": -1, "r2": 0, "r3": 0}
SPLIT_T = ((0, 3), (1, 3))
ON_G = ((1, 3),)
NEG = (2, 3)
PT_ON_V = 0
X0_ON_V = 1


def tile_iwht3layer_pa_kernel(tc, trans, weight, bias, out):
    nc = tc.nc
    x_view = trans.rearrange("t b i j c -> (b i j) t c")
    w_view = weight.rearrange("t (p r) n -> t p r n", r=4)
    out_view = out.rearrange("b (i p) (j q) n -> p q (b i) j n", p=4, q=4)
    bias_row = bias.rearrange("a b c n -> (a b c) n")

    with ExitStack() as ctx:
        sbuf = ctx.enter_context(tc.tile_pool(name="sbuf", bufs=1))
        psum = ctx.enter_context(tc.psum_pool(name="psum", bufs=1))

        ident = sbuf.tile([P, P], F32, name="ident")
        ident_bf = sbuf.tile([P, P], BF16, name="ident_bf")
        ones = sbuf.tile([P, P], BF16, name="ones")
        bias_pad = sbuf.tile([P, K], BF16, name="bias_pad")
        bias_sb = sbuf.tile([P, K], BF16, name="bias_sb")
        x_codes = sbuf.tile([P, 4, 1024], U32, name="x_codes", align_bytes=64)
        x_scales = sbuf.tile([P, 4, 1024], U8, name="x_scales", align_bytes=64)
        make_identity(nc, ident[:])
        if ON_TENSOR:
            make_identity(nc, ident_bf[:])
        nc.gpsimd.memset(bias_pad[:], 0.0)
        nc.gpsimd.memset(ones[:], 1.0)
        ctx.enter_context(tc.manual_schedule())

        raw, grp, wc, ws, x_raw, x_grp = {}, {}, {}, {}, {}, {}
        grp_all = sbuf.tile([P, GRP_BUFS, N, 4], BF16, name="grp_all", align_bytes=64)
        bank_busy = [False] * 8
        written = set()

        def sb(tag, shape, dtype):
            return sbuf.tile(shape, dtype, name=tag, align_bytes=64)

        def bank(b, shape, dtype=F32):
            assert not bank_busy[b], b
            return psum.tile(shape, dtype, name="bank%d" % b)

        def load(item):
            if item == "b":
                nc.sync.dma_start(out=bias_pad[0:1, :], in_=bias_row)
            elif isinstance(item, str):
                c = int(item[1])
                x_raw[c] = sb("x_raw%d" % c, [P, 4, C], BF16)
                nc.sync.dma_start(out=x_raw[c][:], in_=x_view[:, 4 * c : 4 * c + 4, :])
            else:
                h, t = divmod(item, COEFFS)
                raw[item] = sb("raw%d" % (item % RAW_BUFS), [P, 4, N], BF16)
                nc.sync.dma_start(out=raw[item][:], in_=w_view[t, :, :, h * N : (h + 1) * N])

        turned = {}
        pair_at = [0]

        held = {}

        def next_pair(item):
            banks = PAIRS[pair_at[0] % len(PAIRS)]
            pair_at[0] += 1
            held[item] = banks
            return banks

        def pair_free():
            return not any(bank_busy[b] for b in PAIRS[pair_at[0] % len(PAIRS)])

        def hold(item):
            for b in held[item]:
                bank_busy[b] = True

        def release(item):
            for b in held[item]:
                bank_busy[b] = False

        def x_turn(c):
            words = x_raw[c][:].bitcast(F32)
            banks = next_pair("x%d" % c)
            for pair in range(2):
                xt = bank(banks[pair], [P, 2, 2, P])
                turned[c, pair] = xt
                for tt in range(2):
                    for u in range(2):
                        nc.tensor.transpose(xt[:, tt, u, :], words[:, 2 * pair + tt, u : C // 2 : 2], ident[:])

        def x_copy(c):
            x_grp[c] = sb("x_grp%d" % c, [P, 2, 4, C], BF16)
            for pair in range(2):
                copy = nc.vector.tensor_copy if (X0_ON_V and c == 0 and pair == 1) else nc.scalar.copy
                copy(out=x_grp[c][:, 0, 2 * pair : 2 * pair + 2, :].bitcast(F32).rearrange("p t (r u) -> p t r u", u=2),
                     in_=turned[c, pair][:].rearrange("p t u r -> p t r u"))

        def x_quant(c, sign):
            nc.vector.quantize_mx(out=x_codes[:, c, 512 * sign : 512 * sign + 512].bitcast(MX),
                                  scales=x_scales[:, c, 512 * sign : 512 * sign + 512],
                                  in_=x_grp[c][:, sign, :, :].rearrange("p t k -> p (t k)"))

        def x_negate(c):
            nc.vector.tensor_scalar_mul(out=x_grp[c][:, 1, :, :].rearrange("p t k -> p (t k)"),
                                        in0=x_grp[c][:, 0, :, :].rearrange("p t k -> p (t k)"), scalar1=-1.0)

        def bias_mm():
            turned["b"] = bank(next_pair("b")[0], [P, K], BF16)
            for h in range(HALVES):
                nc.tensor.matmul(out=turned["b"][:, h * N : (h + 1) * N], lhsT=ones[:], rhs=bias_pad[:, h * N : (h + 1) * N], start=True, stop=True)

        def bias_copy():
            nc.scalar.copy(out=bias_sb[:], in_=turned["b"][:])
            written.add("b")

        def w_turn(s):
            banks = next_pair(s)
            for i in range(2):
                laid = bank(banks[i], [P, 2 * N], BF16)
                turned["w", s, i] = laid
                for j in range(2):
                    lo = 256 * i + 128 * j
                    nc.tensor.matmul(out=laid[:, N * j : N * (j + 1)], lhsT=ident_bf[:], rhs=raw[s][:, :, lo : lo + 128].rearrange("p r n -> p n r"),
                                     start=True, stop=True)

        def slot(s):
            return grp_all[:, s % GRP_BUFS, :, :]

        def part_copy(s, engine, lo, hi):
            if hi == lo:
                return
            dst, src = slot(s)[:, lo:hi, :], raw[s][:, :, lo:hi].rearrange("p r n -> p n r")
            if engine != "g":
                dst = slot(s)[:, lo:hi, :].rearrange("p (c i) r -> p c r i", i=4)
                src = raw[s][:, :, lo:hi].rearrange("p r (c i) -> p c r i", i=4)
            if engine == "s":
                nc.scalar.copy(out=dst, in_=src)
            elif engine == "g":
                nc.gpsimd.tensor_scalar(out=dst, in0=src, scalar1=1.0, scalar2=0.0, op0=MULT, op1=ADD)
            else:
                nc.vector.tensor_copy(out=dst, in_=src)

        def quantise(s, pieces):
            wc[s] = sb("w_codes%d" % (s % CODE_BUFS), [P, N], U32)
            ws[s] = sb("w_scales%d" % (s % CODE_BUFS), [P, N], U8)
            w = N // pieces
            for i in range(pieces):
                nc.vector.quantize_mx(out=wc[s][:, i * w : (i + 1) * w].bitcast(MX), scales=ws[s][:, i * w : (i + 1) * w],
                                      in_=slot(s)[:, i * w : (i + 1) * w, :].rearrange("p n r -> p (n r)"))

        groups = []
        for h in range(HALVES):
            for q in range(4):
                plus = [4 * u + v for u in range(2) for v in range(4) if HAD[q][v] > 0]
                minus = [4 * u + v for u in range(2) for v in range(4) if HAD[q][v] * (1 - 2 * u) > 0]
                groups.append({"kind": "SA" if q == 0 else "P+", "h": h, "q": q, "bank": q, "panels": [COEFFS * h + t for t in plus], "at": 0, "tile": None})
                groups.append({"kind": "P-", "h": h, "q": q, "bank": 4 + q, "panels": [COEFFS * h + t for t in minus], "at": 0, "tile": None})
            for kind, b0 in (("T+", 0), ("T-", 4)):
                for q in range(4):
                    if (h, q) in SPLIT_T:
                        first = 8 if kind == "T+" else 12
                        groups.append({"kind": "r2" if kind == "T+" else "r3", "h": h, "q": q, "bank": b0 + q, "panels": [COEFFS * h + first + i for i in range(4)], "at": 0, "tile": None})
                        continue
                    groups.append({"kind": kind, "h": h, "q": q, "bank": b0 + q, "panels": [COEFFS * h + 8 + i for i in range(8)], "at": 0, "tile": None})
        turn_at = [0]
        pending = []
        waiting = []
        closed = set()
        part = {}
        z_count = [0]
        z_tiles = {}

        def one_pass(g):
            s = g["panels"][g["at"]]
            t = s % COEFFS
            u, v = divmod(t, 4)
            sign = HAD[g["q"]][v] * (-1 if (g["kind"] == "T-" and u == 3) else 1) if g["kind"][0] in "Tr" else 1
            lo = (0 if sign > 0 else 512) + (t % 4) * P
            nc.tensor.matmul_mx(out=g["tile"][:], lhsT=x_codes[:, t // 4, lo : lo + P].bitcast(MX), lhsT_scale=x_scales[:, t // 4, lo : lo + P],
                                rhs=wc[s][:].bitcast(MX), rhs_scale=ws[s][:], start=g["at"] == 0, stop=g["at"] == len(g["panels"]) - 1)
            g["at"] += 1

        def pe_step(done, last, extra, step):
            left = 1000 if last else (PE_LAST if done >= LAST_FROM else (PE_C0 if 8 <= done < 16 else PE_BUDGET)) + extra
            while left > 0:
                ready = [g for g in groups if g["at"] < len(g["panels"]) and g["panels"][g["at"]] <= done
                         and (g["panels"][g["at"]] % COEFFS) // 4 in written and (g["tile"] is not None or (not bank_busy[g["bank"]] and (g["bank"] < 4 or turn_at[0] >= len(SEQ_HEAD))))]
                if not ready:
                    break
                g = min(ready, key=lambda g: (g["h"], RANK[g["kind"]], g["q"], g["panels"][g["at"]]))
                if g["tile"] is None:
                    g["tile"] = bank(g["bank"], [P, N])
                    bank_busy[g["bank"]] = True
                one_pass(g)
                left -= 1
                if g["at"] == len(g["panels"]):
                    if g["kind"][0] == "P":
                        (pending if ("SA", g["h"]) in closed else waiting).append((g, 1, step))
                    elif g["kind"][0] == "r":
                        pending.extend([(g, 0, step)] if (g["h"], g["q"]) in ON_G else [(g, i, step) for i in range(4)])
                    else:
                        pending.extend([(g, -1, step), (g, 1, step)] if g["kind"] == "SA" else [(g, 1, step), (g, -1, step)])
                        if g["kind"] == "SA":
                            closed.add(("SA", g["h"]))
                            pending.extend([(e[0], e[1], step) for e in sorted(waiting, key=lambda e: (RANK[e[0]["kind"]], e[0]["q"]))])
                            waiting.clear()

        def combine(dst, src, factor, other):
            nc.vector.scalar_tensor_tensor(out=dst, in0=src[:], scalar=factor, in1=other, op0=MULT, op1=ADD)

        def result_tile():
            k = z_count[0] % 16
            z_count[0] += 1
            if k % 4 == 0:
                z_tiles[k // 4] = sb("x_grp%d" % (k // 4), [P, 4, N], F32)
            return z_tiles[k // 4][:, k % 4, :]

        def epilogue(g, sg):
            h, q, kind = g["h"], g["q"], g["kind"]
            if kind == "SA":
                key = ("c", h) if sg < 0 else ("f", h, 0, 1)
                part[key] = sb("c_all" if sg < 0 else "f0_2", [P, N], F32)
                combine(part[key][:], g["tile"], sg / 16.0, bias_sb[:, h * N : (h + 1) * N])
                if sg > 0:
                    bank_busy[g["bank"]] = False
            elif kind[0] == "P":
                a = 1 if kind == "P+" else -1
                part["f", h, q, a] = sb("f%d_%d" % (q, a + 1), [P, N], F32)
                combine(part["f", h, q, a][:], g["tile"], 1.0 / 8, part["c", h][:])
                bank_busy[g["bank"]] = False
            elif kind in ("r2", "r3") and (h, q) not in ON_G:
                a = 1 if sg % 2 == 0 else -1
                if kind == "r2":
                    part["e", h, q, sg] = sb("e%d_%d" % (q, sg), [P, N], F32)
                    combine(part["e", h, q, sg][:], g["tile"], HAD[sg][2] / 16.0, part["f", h, q, a][:])
                else:
                    z = result_tile()
                    combine(z, g["tile"], HAD[sg][3] / 16.0, part["e", h, q, sg][:])
                    nc.sync.dma_start(out=out_view[sg, q, :, :, h * N : (h + 1) * N], in_=z)
                if sg == 3:
                    bank_busy[g["bank"]] = False
            elif kind in ("r2", "r3"):
                part[kind, h, q] = sb("%s_%d" % (kind, q), [P, N], F32)
                nc.scalar.activation(out=part[kind, h, q][:], in_=g["tile"][:], func=COPY, scale=1.0 / 16)
                bank_busy[g["bank"]] = False
                if kind == "r3":
                    for a in (1, -1):
                        b = sb("b%d_%d" % (q, a + 1), [P, N], F32)
                        nc.gpsimd.tensor_tensor(out=b[:], in0=part["r2", h, q][:], in1=part["r3", h, q][:], op=ADD if a > 0 else SUB)
                        for s2 in (1, -1):
                            z = result_tile()
                            nc.gpsimd.tensor_tensor(out=z, in0=part["f", h, q, a][:], in1=b[:], op=ADD if s2 > 0 else SUB)
                            nc.scalar.dma_start(out=out_view[(0 if a > 0 else 1) + (0 if s2 > 0 else 2), q, :, :, h * N : (h + 1) * N], in_=z)
            else:
                a = 1 if kind == "T+" else -1
                z = result_tile()
                combine(z, g["tile"], sg / 16.0, part["f", h, q, a][:])
                nc.sync.dma_start(out=out_view[(0 if a > 0 else 1) + (0 if sg > 0 else 2), q, :, :, h * N : (h + 1) * N], in_=z)
                if sg < 0:
                    bank_busy[g["bank"]] = False

        def on_vector(e):
            return e[0]["kind"] not in ("r2", "r3") or (e[0]["h"], e[0]["q"]) not in ON_G

        items = list(SEQ_HEAD) + [s for s in range(PANELS) if s not in SEQ_HEAD]
        n_items = len(items)
        panel_step = {}
        for k in range(n_items):
            panel_step[items[k]] = k
        for item in items[:LOADS_AHEAD]:
            load(item)

        def is_x(item):
            return isinstance(item, str) and item != "b"

        def turns(upto):
            while turn_at[0] < min(upto, n_items):
                item = items[turn_at[0]]
                if isinstance(item, str) or item in ON_TENSOR:
                    if not pair_free():
                        break
                    if is_x(item):
                        x_turn(int(item[1]))
                    elif item == "b":
                        bias_mm()
                    else:
                        w_turn(item)
                    hold(item)
                turn_at[0] += 1

        g_cols = {}
        v_cols = {}

        def spread_s(k):
            if 0 <= k < n_items:
                item = items[k]
                assert turn_at[0] > k
                if item == "b":
                    bias_copy()
                    release(item)
                elif is_x(item):
                    x_copy(int(item[1]))
                    release(item)
                elif item in ON_TENSOR:
                    for i in range(2):
                        copy = nc.vector.tensor_copy if (PT_ON_V and i == 1) else nc.scalar.copy
                        copy(out=slot(item)[:, 256 * i : 256 * (i + 1), :].rearrange("p n r -> p (n r)"), in_=turned["w", item, i][:])
                    release(item)
                else:
                    part_copy(item, "s", g_cols.get(item, 0), N - v_cols[item])

        def spread_v(k, n_epi, x_work, when):
            if 0 <= k < n_items and not isinstance(items[k], str) and items[k] not in ON_TENSOR:
                v_cols[items[k]] = N - g_cols.get(items[k], 0) - (S_COLS_X if x_work else S_COLS[min(n_epi, 2)])
                if when == (v_cols[items[k]] <= V_SMALL or n_epi == 0) and v_cols[items[k]] > 0:
                    part_copy(items[k], "v", N - v_cols[items[k]], N)

        def spread_g(s, n_epi):
            if s < PANELS and s not in ON_TENSOR and G_COLS[min(n_epi, 2)]:
                g_cols[s] = G_COLS[min(n_epi, 2)]
                part_copy(s, "g", 0, g_cols[s])

        late = []

        def stage2(item, pieces):
            todo = list(late)
            late.clear()
            if is_x(item):
                x_quant(int(item[1]), 0)
                if int(item[1]) in NEG:
                    x_negate(int(item[1]))
                    late.append(int(item[1]))
                else:
                    written.add(int(item[1]))
            elif item != "b":
                quantise(item, pieces)
            for c in todo:
                x_quant(c, 1)
                written.add(c)

        for k in range(LEAD):
            turns(k + LEAD_T)
            spread_v(k, 0, True, True)
            spread_s(k)
        k = 0
        done = -1
        n_epi = 0
        while k < n_items or pending or any(g["at"] < len(g["panels"]) for g in groups):
            last = k >= n_items - 1
            item = items[k] if k < n_items else None
            turns(k + LEAD + LEAD_T)
            x_work = bool(late) or (item is not None and is_x(item))
            ahead = len([e for e in pending if e[2] + LAG <= k and on_vector(e)])
            if item is not None:
                stage2(item, SPLIT_Q if (ahead and not last and "b" in written) else 1)
                if not isinstance(item, str):
                    done = item
            pe_step(done, last, n_epi, k)
            ripe = 0
            for e in pending:
                if "b" not in written or (e[2] + LAG > k and not last):
                    break
                ripe += 1
            burst = len([e for e in pending[:ripe] if e[0]["kind"] in BURST])
            n_epi = ripe if last else max(min(V_EPI, ripe), min(burst, V_BURST))
            n_v = len([e for e in pending[:n_epi] if on_vector(e)])
            if item is not None and not isinstance(item, str):
                spread_g(item + LEAD_G, n_v)
            spread_v(k + LEAD, n_v, x_work, True)
            spread_s(k + LEAD)
            if k + LOADS_AHEAD < n_items:
                load(items[k + LOADS_AHEAD])
            for i in range(n_epi):
                g, sg, at_step = pending.pop(0)
                epilogue(g, sg)
            spread_v(k + LEAD, n_v, x_work, False)
            k += 1
